import numpy as np
import ml_dtypes


def mxq(x, axis, fmt="e4m3"):
    dtype, down = {"e4m3": (ml_dtypes.float8_e4m3fn, 7), "e5m2": (ml_dtypes.float8_e5m2, 14)}[fmt]
    v = np.moveaxis(np.asarray(x, np.float32).astype(ml_dtypes.bfloat16).astype(np.float64), axis, -1)
    blocks = v.reshape(v.shape[:-1] + (-1, 32))
    amax = np.abs(blocks).max(-1, keepdims=True)
    byte = np.maximum(np.where(amax > 0, np.frexp(amax)[1] - 1 + 127, 0) - down, 1)
    scale = np.exp2(byte - 127.0)
    codes = (blocks / scale).astype(np.float32).astype(dtype).astype(np.float64)
    return np.moveaxis((codes * scale).reshape(v.shape), -1, axis)


WIDE = False


def mx_kscale(k):
    if not WIDE:
        return np.ones(k)
    levels = np.array([10, -10, 5, -5, 0])
    a = np.random.permutation(np.resize(levels, k // 512 * 4)).reshape(k // 512, 4)
    idx = np.arange(k)
    return np.exp2(a[idx // 512, idx % 128 // 32])


BF16 = ml_dtypes.bfloat16


def bf(x):
    return np.asarray(x, np.float32).astype(BF16)


def f64(x):
    return np.asarray(x).astype(np.float64)


E2M1 = np.array([0.0, 0.5, 1.0, 1.5, 2.0, 3.0, 4.0, 6.0, -0.0, -0.5, -1.0, -1.5, -2.0, -3.0, -4.0, -6.0])


def pack_weight(w, fmt):
    k, n = w.shape
    w = f64(bf(w)).reshape(k // 32, 32, n)
    amax = np.abs(w).max(1)
    if fmt == "e4m3":
        byte = np.frexp(amax)[1] - 1 + 127 - 7
    else:
        mant, ex = np.frexp(amax / 6.0)
        byte = np.where(mant > 0.5, ex, ex - 1) + 127
    byte = np.clip(np.where(amax > 0, byte, 1), 1, 254)
    scaled = (w * np.exp2(127.0 - byte)[:, None, :]).reshape(k, n).astype(np.float32)
    by_word = np.ascontiguousarray(scaled.reshape(k // 512, 128, 4, n).transpose(0, 1, 3, 2))
    if fmt == "e4m3":
        words = by_word.astype(ml_dtypes.float8_e4m3fn).view(np.uint8)
    else:
        c = by_word.astype(ml_dtypes.float4_e2m1fn).view(np.uint8) & 0xF
        words = c[..., 0::2] | (c[..., 1::2] << 4)
    return np.ascontiguousarray(words), np.ascontiguousarray(byte.astype(np.uint8).reshape(k // 512, 16, n))


def unpack_weight(words, scales, fmt):
    g, p, n, _ = words.shape
    if fmt == "e4m3":
        vals = np.ascontiguousarray(words).view(ml_dtypes.float8_e4m3fn).astype(np.float64)
    else:
        nib = np.empty((g, p, n, 4), np.uint8)
        nib[..., 0::2] = words & 0xF
        nib[..., 1::2] = words >> 4
        vals = E2M1[nib]
    vals = vals * np.repeat(np.exp2(scales.astype(np.float64) - 127.0), 8, axis=1)[..., None]
    return vals.transpose(0, 1, 3, 2).reshape(g * 512, n)


B, T, D, O = 128, 32, 512, 512


def erf(z):
    a = np.clip(z, -6.0, 6.0)
    q = 2.0 * a * a
    term = a.copy()
    total = a.copy()
    for k in range(1, 130):
        term = term * q / (2 * k + 1)
        total = total + term
    return 2.0 / np.sqrt(np.pi) * np.exp(-a * a) * total


def gelu_exact(v):
    return 0.5 * v * (1.0 + erf(v / np.sqrt(2.0)))


def setup_inputs():
    s = mx_kscale(D)
    x = np.random.standard_normal((B, T, D)) * s
    lengths = np.random.randint(T // 4, T + 1, size=B)
    lengths[np.random.randint(B)] = T
    pad = np.arange(T)[None, :] >= lengths[:, None]
    x = np.where(pad[:, :, None], -1.0, x)
    w = np.random.standard_normal((O, D)) / np.sqrt(D) / s[None, :]
    words, scales = pack_weight(np.ascontiguousarray(w.T), "e4m3")
    return {"x": bf(x), "W_words": words, "W_scales": scales, "b": bf(np.random.standard_normal(O) * 0.3)}


def reference(x, W_words, W_scales, b):
    x = f64(x)
    valid = ~np.all(x == -1.0, axis=-1)
    y = gelu_exact((mxq(x, 2, "e4m3") @ unpack_weight(W_words, W_scales, "e4m3")) + f64(b))
    vf = valid[..., None].astype(np.float64)
    n = np.sum(vf, axis=1)
    mean = np.sum(y * vf, axis=1) / n
    diff = (y - mean[:, None, :]) * vf
    var = np.sum(diff * diff, axis=1) / np.maximum(n - 1.0, 1.0)
    std = np.where(n > 1.0, np.sqrt(var), np.zeros_like(var))
    out = np.concatenate([std, mean], axis=-1)
    return np.where(np.isnan(out), np.zeros_like(out), out)

@@ -1,0 +1,270 @@
+from contextlib import ExitStack
+
+import concourse.mybir as mybir
+from concourse.masks import make_identity
+
+F32 = mybir.dt.float32
+BF16 = mybir.dt.bfloat16
+I32 = mybir.dt.int32
+U32 = mybir.dt.uint32
+U8 = mybir.dt.uint8
+FP8X4 = mybir.dt.float8_e4m3fn_x4
+ACT = mybir.ActivationFunctionType
+ALU = mybir.AluOpType
+AX = mybir.AxisListType
+
+P = 128
+SAMPLES = 128
+TOKENS = 32
+K = 512
+FEATURES = 512
+F_TILES = FEATURES // P
+WORDS = K // 2
+
+GROUP_ROWS = 512
+GROUPS = SAMPLES * TOKENS // GROUP_ROWS
+GROUP_SAMPLES = GROUP_ROWS // TOKENS
+ROWS_PER_PARTITION = GROUP_ROWS // P
+PARTITIONS_PER_SAMPLE = TOKENS // ROWS_PER_PARTITION
+
+PAD_WORD = -(1.0 + 0xBF80 / 2.0**23)
+
+FLOPS = 2 * SAMPLES * TOKENS * K * FEATURES
+
+
+def tile_linearnnencoder_kernel(tc, x, W_words, W_scales, b, out):
+    nc = tc.nc
+    rows = x.flatten_outer_dims()
+
+    with ExitStack() as pools:
+        const = pools.enter_context(tc.tile_pool(name="const", bufs=1))
+        stage = pools.enter_context(tc.tile_pool(name="stage", bufs=3))
+        acts = pools.enter_context(tc.tile_pool(name="acts", bufs=4))
+        psum_x = pools.enter_context(tc.psum_pool(name="psum_x", bufs=2))
+        psum_z = pools.enter_context(tc.psum_pool(name="psum_z", bufs=3))
+        psum_small = pools.enter_context(tc.psum_pool(name="psum_small", bufs=1))
+
+        zero_col = const.tile([P, 1], F32)
+        nc.vector.memset(zero_col[:], 0.0)
+        warm_col = const.tile([P, 1], F32)
+        nc.scalar.activation(out=warm_col[:], in_=zero_col[:], func=ACT.Gelu)
+
+        x_all = const.tile([P, GROUPS, ROWS_PER_PARTITION * K], BF16)
+
+        def load_x(g):
+            nc.sync.dma_start(
+                out=x_all[:, g, :],
+                in_=rows[g * GROUP_ROWS : (g + 1) * GROUP_ROWS, :].rearrange(
+                    "(p r) k -> p (r k)", r=ROWS_PER_PARTITION
+                ),
+            )
+
+        load_x(0)
+
+        w_codes = const.tile([P, FEATURES * 4], U8, align_bytes=64)
+        nc.sync.dma_start(
+            out=w_codes[:].bitcast(I32),
+            in_=W_words.rearrange("o p n t -> p (o n t)").bitcast(I32),
+        )
+        w_plane = const.tile([P, FEATURES], U8, align_bytes=64)
+        nc.vector.memset(w_plane[:].bitcast(I32), 0)
+        for quadrant in range(4):
+            nc.sync.dma_start(
+                out=w_plane[32 * quadrant : 32 * quadrant + 4, :].bitcast(I32),
+                in_=W_scales[0, 4 * quadrant : 4 * quadrant + 4, :].bitcast(I32),
+            )
+        bias_rows_bf = const.tile([P, P], BF16)
+        nc.vector.memset(bias_rows_bf[:], 0.0)
+        nc.sync.dma_start(out=bias_rows_bf[0:F_TILES, :], in_=b.rearrange("(f c) -> f c", f=F_TILES))
+
+        for g in range(1, GROUPS):
+            load_x(g)
+        bias_everywhere = const.tile([P, FEATURES], BF16)
+        nc.sync.dma_start(out=bias_everywhere[:], in_=b.partition_broadcast(P))
+
+        ident = const.tile([P, P], F32)
+        make_identity(nc, ident[:])
+        sample_of = const.tile([P, GROUP_SAMPLES], F32)
+        nc.vector.tensor_reduce(
+            out=sample_of[:],
+            in_=ident[:].rearrange("p (s h) -> p s h", h=PARTITIONS_PER_SAMPLE),
+            axis=AX.X,
+            op=ALU.add,
+        )
+        ones_bf = const.tile([P, 32], BF16)
+        nc.vector.memset(ones_bf[:], 1.0)
+        minus_pad_word = const.tile([P, 1], F32)
+        nc.vector.memset(minus_pad_word[:], -PAD_WORD)
+
+        bias_rows = const.tile([P, P], F32)
+        nc.vector.tensor_copy(out=bias_rows[:], in_=bias_rows_bf[:])
+        bias_ps = psum_small.tile([P, P], F32, tag="small")
+        nc.tensor.transpose(bias_ps[:], bias_rows[:], ident[:])
+        bias = const.tile([P, F_TILES], F32)
+        nc.vector.tensor_copy(out=bias[:], in_=bias_ps[:, 0:F_TILES])
+
+        def w_tile(f):
+            return dict(
+                lhsT=w_codes[:, f * P * 4 : (f + 1) * P * 4].bitcast(FP8X4),
+                lhsT_scale=w_plane[:, f * P : (f + 1) * P],
+            )
+
+        stats = const.tile([P, F_TILES, 3, SAMPLES], F32)
+        distance = const.tile([P, GROUPS, ROWS_PER_PARTITION], F32)
+
+        def prepare(g):
+            x_words = x_all[:, g, :].bitcast(F32)
+
+            for r in range(ROWS_PER_PARTITION):
+                squares = acts.tile([P, WORDS], BF16)
+                nc.scalar.activation(
+                    out=squares[:],
+                    in_=x_words[:, r * WORDS : (r + 1) * WORDS],
+                    func=ACT.Square,
+                    bias=minus_pad_word[:],
+                    accum_out=distance[:, g, r : r + 1],
+                )
+
+            xt_v = psum_x.tile([P, 2, 2, P], F32)
+            xt_s = psum_x.tile([P, 2, 2, P], F32)
+            for r in range(ROWS_PER_PARTITION):
+                keep_row = stage.tile([P, P], F32, bufs=4)
+                nc.vector.tensor_scalar(
+                    out=keep_row[:],
+                    in0=ident[:],
+                    scalar1=distance[:, g, r : r + 1],
+                    scalar2=0.0,
+                    op0=ALU.mult,
+                    op1=ALU.is_gt,
+                )
+                xt = xt_v if r < 2 else xt_s
+                for u in range(2):
+                    nc.tensor.transpose(
+                        xt[:, r % 2, u, :],
+                        x_words[:, r * WORDS + u : (r + 1) * WORDS : 2],
+                        keep_row[:],
+                    )
+            grouped = stage.tile([P, ROWS_PER_PARTITION, P, 4], BF16, align_bytes=64)
+            grouped_words = grouped[:].bitcast(F32)
+            nc.vector.tensor_copy(out=grouped_words[:, 0:2, :, :], in_=xt_v[:].rearrange("j r u p -> j r p u"))
+            nc.scalar.copy(out=grouped_words[:, 2:4, :, :], in_=xt_s[:].rearrange("j r u p -> j r p u"))
+            x_codes = stage.tile([P, GROUP_ROWS], U32, align_bytes=64)
+            x_plane = stage.tile([P, GROUP_ROWS], U8, align_bytes=64)
+            nc.vector.quantize_mx(
+                out=x_codes[:].bitcast(FP8X4),
+                scales=x_plane[:],
+                in_=grouped[:].rearrange("j r p t -> j (r p t)"),
+            )
+            return x_codes, x_plane
+
+        def consume(g, x_codes, x_plane):
+            for f in range(F_TILES):
+                z = psum_z.tile([P, GROUP_ROWS], F32)
+                nc.tensor.matmul_mx(
+                    out=z[:],
+                    rhs=x_codes[:].bitcast(FP8X4),
+                    rhs_scale=x_plane[:],
+                    start=True,
+                    stop=True,
+                    **w_tile(f),
+                )
+                y = acts.tile([P, GROUP_ROWS], F32)
+                nc.scalar.activation(out=y[:], in_=z[:], func=ACT.Gelu, bias=bias[:, f : f + 1])
+                y_by_sample = y[:].rearrange(
+                    "o (r s h) -> o r s h", r=ROWS_PER_PARTITION, s=GROUP_SAMPLES
+                )
+                for pair in range(GROUP_SAMPLES // 2):
+                    s = g * GROUP_SAMPLES + 2 * pair
+                    nc.vector.bn_stats(
+                        out=stats[:, f, :, s : s + 2].rearrange("o kind e -> o e kind"),
+                        in_=y_by_sample[:, :, 2 * pair : 2 * pair + 2, :].rearrange("o r e h -> o r h e"),
+                    )
+
+        ready = prepare(0)
+        for g in range(GROUPS):
+            current = ready
+            if g + 1 < GROUPS:
+                ready = prepare(g + 1)
+            consume(g, *current)
+
+        pad_y = const.tile([P, FEATURES], F32)
+        nc.scalar.activation(out=pad_y[:], in_=bias_everywhere[:], func=ACT.Gelu)
+
+        is_pad = const.tile([P, GROUPS, ROWS_PER_PARTITION], F32)
+        nc.vector.tensor_single_scalar(out=is_pad[:], in_=distance[:], scalar=0.0, op=ALU.is_equal)
+        pads_here = const.tile([P, GROUPS], F32)
+        nc.vector.tensor_reduce(out=pads_here[:], in_=is_pad[:], axis=AX.X, op=ALU.add)
+        spread = const.tile([P, GROUPS, GROUP_SAMPLES], BF16)
+        nc.vector.tensor_tensor(
+            out=spread[:],
+            in0=pads_here[:].unsqueeze(2).to_broadcast([P, GROUPS, GROUP_SAMPLES]),
+            in1=sample_of[:].unsqueeze(1).to_broadcast([P, GROUPS, GROUP_SAMPLES]),
+            op=ALU.mult,
+        )
+        pads_ps = psum_small.tile([P, 32], F32, tag="small")
+        nc.tensor.matmul(
+            out=pads_ps[:], lhsT=spread[:].rearrange("p g s -> p (g s)"), rhs=ones_bf[:], start=True, stop=True
+        )
+
+        def column(name):
+            return const.tile([P, 1], F32, name=name)
+
+        pads = column("pads")
+        nc.vector.tensor_copy(out=pads[:], in_=pads_ps[:, 0:1])
+        n = column("n")
+        nc.vector.tensor_scalar(out=n[:], in0=pads[:], scalar1=-1.0, scalar2=float(TOKENS), op0=ALU.mult, op1=ALU.add)
+        inv_n = column("inv_n")
+        nc.vector.tensor_scalar_max(out=inv_n[:], in0=n[:], scalar1=1.0)
+        nc.vector.reciprocal(out=inv_n[:], in_=inv_n[:])
+        some = column("some")
+        nc.vector.tensor_scalar_min(out=some[:], in0=n[:], scalar1=1.0)
+        nc.vector.tensor_mul(out=inv_n[:], in0=inv_n[:], in1=some[:])
+        all_over_n = column("all_over_n")
+        nc.vector.tensor_scalar_mul(out=all_over_n[:], in0=inv_n[:], scalar1=float(TOKENS))
+        pads_over_n = column("pads_over_n")
+        nc.vector.tensor_mul(out=pads_over_n[:], in0=pads[:], in1=inv_n[:])
+        shift_weight = column("shift_weight")
+        nc.vector.tensor_scalar_mul(out=shift_weight[:], in0=pads_over_n[:], scalar1=float(TOKENS))
+        n_less_1 = column("n_less_1")
+        nc.vector.tensor_scalar(out=n_less_1[:], in0=n[:], scalar1=-1.0, scalar2=0.0, op0=ALU.add, op1=ALU.max)
+        inv_n_less_1 = column("inv_n_less_1")
+        nc.vector.tensor_scalar_max(out=inv_n_less_1[:], in0=n_less_1[:], scalar1=1.0)
+        nc.vector.reciprocal(out=inv_n_less_1[:], in_=inv_n_less_1[:])
+        several = column("several")
+        nc.vector.tensor_scalar_min(out=several[:], in0=n_less_1[:], scalar1=1.0)
+        nc.vector.tensor_mul(out=inv_n_less_1[:], in0=inv_n_less_1[:], in1=several[:])
+
+        mean_all = psum_x.tile([P, F_TILES, P], F32, tag="xt_v")
+        m2_all = psum_x.tile([P, F_TILES, P], F32, tag="xt_s")
+        for f in range(F_TILES):
+            nc.tensor.transpose(mean_all[:, f, :], stats[:, f, 1, :], ident[:])
+        for f in range(F_TILES):
+            nc.tensor.transpose(m2_all[:, f, :], stats[:, f, 2, :], ident[:])
+        mean_all_flat = mean_all[:].rearrange("s f o -> s (f o)")
+        m2_all_flat = m2_all[:].rearrange("s f o -> s (f o)")
+
+        result = const.tile([P, 2 * FEATURES], F32)
+
+        gap = const.tile([P, FEATURES], F32)
+        nc.vector.tensor_tensor(out=gap[:], in0=mean_all_flat, in1=pad_y[:], op=ALU.subtract)
+        shift = const.tile([P, FEATURES], F32)
+        nc.vector.scalar_tensor_tensor(
+            out=shift[:], in0=gap[:], scalar=shift_weight[:], in1=gap[:], op0=ALU.mult, op1=ALU.mult
+        )
+        m2_valid = const.tile([P, FEATURES], F32)
+        nc.vector.tensor_tensor(out=m2_valid[:], in0=m2_all_flat, in1=shift[:], op=ALU.subtract)
+        nc.vector.tensor_scalar_max(out=m2_valid[:], in0=m2_valid[:], scalar1=0.0)
+        nc.scalar.activation(out=result[:, 0:FEATURES], in_=m2_valid[:], func=ACT.Sqrt, scale=inv_n_less_1[:])
+        nc.sync.dma_start(out=out[:, 0:FEATURES], in_=result[:, 0:FEATURES])
+
+        pad_part = const.tile([P, FEATURES], F32)
+        nc.vector.tensor_scalar_mul(out=pad_part[:], in0=pad_y[:], scalar1=pads_over_n[:])
+        nc.vector.scalar_tensor_tensor(
+            out=result[:, FEATURES : 2 * FEATURES],
+            in0=mean_all_flat,
+            scalar=all_over_n[:],
+            in1=pad_part[:],
+            op0=ALU.mult,
+            op1=ALU.subtract,
+        )
+        nc.sync.dma_start(out=out[:, FEATURES : 2 * FEATURES], in_=result[:, FEATURES : 2 * FEATURES])

@@ -109,7 +109,7 @@ def tile_linearnnencoder_kernel(tc, x, W_words, W_scales, b, out):
                 lhsT_scale=w_plane[:, f * P : (f + 1) * P],
             )
 
-        stats = const.tile([P, F_TILES, 3, SAMPLES], F32)
+        stats = const.tile([P, F_TILES, SAMPLES, 3], F32)
         distance = const.tile([P, GROUPS, ROWS_PER_PARTITION], F32)
 
         def prepare(g):
@@ -176,7 +176,7 @@ def tile_linearnnencoder_kernel(tc, x, W_words, W_scales, b, out):
                 for pair in range(GROUP_SAMPLES // 2):
                     s = g * GROUP_SAMPLES + 2 * pair
                     nc.vector.bn_stats(
-                        out=stats[:, f, :, s : s + 2].rearrange("o kind e -> o e kind"),
+                        out=stats[:, f, s : s + 2, :].rearrange("o e kind -> o (e kind)"),
                         in_=y_by_sample[:, :, 2 * pair : 2 * pair + 2, :].rearrange("o r e h -> o r h e"),
                     )
 
@@ -237,9 +237,9 @@ def tile_linearnnencoder_kernel(tc, x, W_words, W_scales, b, out):
         mean_all = psum_x.tile([P, F_TILES, P], F32, tag="xt_v")
         m2_all = psum_x.tile([P, F_TILES, P], F32, tag="xt_s")
         for f in range(F_TILES):
-            nc.tensor.transpose(mean_all[:, f, :], stats[:, f, 1, :], ident[:])
+            nc.tensor.transpose(mean_all[:, f, :], stats[:, f, :, 1], ident[:])
         for f in range(F_TILES):
-            nc.tensor.transpose(m2_all[:, f, :], stats[:, f, 2, :], ident[:])
+            nc.tensor.transpose(m2_all[:, f, :], stats[:, f, :, 2], ident[:])
         mean_all_flat = mean_all[:].rearrange("s f o -> s (f o)")
         m2_all_flat = m2_all[:].rearrange("s f o -> s (f o)")
 

@@ -36,18 +36,22 @@ def tile_linearnnencoder_kernel(tc, x, W_words, W_scales, b, out):
     nc = tc.nc
     rows = x.flatten_outer_dims()
 
-    with ExitStack() as pools:
-        const = pools.enter_context(tc.tile_pool(name="const", bufs=1))
-        stage = pools.enter_context(tc.tile_pool(name="stage", bufs=3))
-        acts = pools.enter_context(tc.tile_pool(name="acts", bufs=4))
-        psum_x = pools.enter_context(tc.psum_pool(name="psum_x", bufs=2))
-        psum_z = pools.enter_context(tc.psum_pool(name="psum_z", bufs=3))
-        psum_small = pools.enter_context(tc.psum_pool(name="psum_small", bufs=1))
+    with ExitStack() as scopes:
+        const = scopes.enter_context(tc.tile_pool(name="const", bufs=1))
+        stage = scopes.enter_context(tc.tile_pool(name="stage", bufs=3))
+        acts = scopes.enter_context(tc.tile_pool(name="acts", bufs=4))
+        psum_x = scopes.enter_context(tc.psum_pool(name="psum_x", bufs=2))
+        psum_z = scopes.enter_context(tc.psum_pool(name="psum_z", bufs=4))
+        scopes.enter_context(tc.manual_schedule())
 
         zero_col = const.tile([P, 1], F32)
         nc.vector.memset(zero_col[:], 0.0)
         warm_col = const.tile([P, 1], F32)
         nc.scalar.activation(out=warm_col[:], in_=zero_col[:], func=ACT.Gelu)
+
+        bias_rows_bf = const.tile([P, P], BF16)
+        nc.vector.memset(bias_rows_bf[:], 0.0)
+        nc.sync.dma_start(out=bias_rows_bf[0:F_TILES, :], in_=b.rearrange("(f c) -> f c", f=F_TILES))
 
         x_all = const.tile([P, GROUPS, ROWS_PER_PARTITION * K], BF16)
 
@@ -60,7 +64,7 @@ def tile_linearnnencoder_kernel(tc, x, W_words, W_scales, b, out):
             )
 
         load_x(0)
-
+        load_x(1)
         w_codes = const.tile([P, FEATURES * 4], U8, align_bytes=64)
         nc.sync.dma_start(
             out=w_codes[:].bitcast(I32),
@@ -73,17 +77,22 @@ def tile_linearnnencoder_kernel(tc, x, W_words, W_scales, b, out):
                 out=w_plane[32 * quadrant : 32 * quadrant + 4, :].bitcast(I32),
                 in_=W_scales[0, 4 * quadrant : 4 * quadrant + 4, :].bitcast(I32),
             )
-        bias_rows_bf = const.tile([P, P], BF16)
-        nc.vector.memset(bias_rows_bf[:], 0.0)
-        nc.sync.dma_start(out=bias_rows_bf[0:F_TILES, :], in_=b.rearrange("(f c) -> f c", f=F_TILES))
-
-        for g in range(1, GROUPS):
+        for g in range(2, GROUPS):
             load_x(g)
         bias_everywhere = const.tile([P, FEATURES], BF16)
         nc.sync.dma_start(out=bias_everywhere[:], in_=b.partition_broadcast(P))
 
         ident = const.tile([P, P], F32)
         make_identity(nc, ident[:])
+        minus_pad_word = const.tile([P, 1], F32)
+        nc.vector.memset(minus_pad_word[:], -PAD_WORD)
+        ones_bf = const.tile([P, 32], BF16)
+        nc.vector.memset(ones_bf[:], 1.0)
+        minus_ones = const.tile([P, 2], F32)
+        nc.vector.memset(minus_ones[:], -1.0)
+        zero_and_one = const.tile([P, 2], F32)
+        nc.vector.memset(zero_and_one[:, 0:1], 0.0)
+        nc.vector.memset(zero_and_one[:, 1:2], 1.0)
         sample_of = const.tile([P, GROUP_SAMPLES], F32)
         nc.vector.tensor_reduce(
             out=sample_of[:],
@@ -91,63 +100,65 @@ def tile_linearnnencoder_kernel(tc, x, W_words, W_scales, b, out):
             axis=AX.X,
             op=ALU.add,
         )
-        ones_bf = const.tile([P, 32], BF16)
-        nc.vector.memset(ones_bf[:], 1.0)
-        minus_pad_word = const.tile([P, 1], F32)
-        nc.vector.memset(minus_pad_word[:], -PAD_WORD)
 
         bias_rows = const.tile([P, P], F32)
         nc.vector.tensor_copy(out=bias_rows[:], in_=bias_rows_bf[:])
-        bias_ps = psum_small.tile([P, P], F32, tag="small")
+        bias_ps = psum_z.tile([P, P], F32, tag="z")
         nc.tensor.transpose(bias_ps[:], bias_rows[:], ident[:])
         bias = const.tile([P, F_TILES], F32)
         nc.vector.tensor_copy(out=bias[:], in_=bias_ps[:, 0:F_TILES])
 
-        def w_tile(f):
-            return dict(
-                lhsT=w_codes[:, f * P * 4 : (f + 1) * P * 4].bitcast(FP8X4),
-                lhsT_scale=w_plane[:, f * P : (f + 1) * P],
-            )
-
         stats = const.tile([P, F_TILES, SAMPLES, 3], F32)
         distance = const.tile([P, GROUPS, ROWS_PER_PARTITION], F32)
 
-        def prepare(g):
-            x_words = x_all[:, g, :].bitcast(F32)
+        def x_words(g):
+            return x_all[:, g, :].bitcast(F32)
 
+        def test_padding(g):
             for r in range(ROWS_PER_PARTITION):
                 squares = acts.tile([P, WORDS], BF16)
                 nc.scalar.activation(
                     out=squares[:],
-                    in_=x_words[:, r * WORDS : (r + 1) * WORDS],
+                    in_=x_words(g)[:, r * WORDS : (r + 1) * WORDS],
                     func=ACT.Square,
                     bias=minus_pad_word[:],
                     accum_out=distance[:, g, r : r + 1],
                 )
 
-            xt_v = psum_x.tile([P, 2, 2, P], F32)
-            xt_s = psum_x.tile([P, 2, 2, P], F32)
+        def keep_valid_rows(g):
+            keep_rows = stage.tile([P, ROWS_PER_PARTITION, P], F32, bufs=2)
             for r in range(ROWS_PER_PARTITION):
-                keep_row = stage.tile([P, P], F32, bufs=4)
                 nc.vector.tensor_scalar(
-                    out=keep_row[:],
+                    out=keep_rows[:, r, :],
                     in0=ident[:],
                     scalar1=distance[:, g, r : r + 1],
                     scalar2=0.0,
                     op0=ALU.mult,
                     op1=ALU.is_gt,
                 )
+            return keep_rows
+
+        def transpose_rows(g, keep_rows):
+            xt_v = psum_x.tile([P, 2, 2, P], F32)
+            xt_s = psum_x.tile([P, 2, 2, P], F32)
+            for r in range(ROWS_PER_PARTITION):
                 xt = xt_v if r < 2 else xt_s
                 for u in range(2):
                     nc.tensor.transpose(
                         xt[:, r % 2, u, :],
-                        x_words[:, r * WORDS + u : (r + 1) * WORDS : 2],
-                        keep_row[:],
+                        x_words(g)[:, r * WORDS + u : (r + 1) * WORDS : 2],
+                        keep_rows[:, r, :],
                     )
+            return xt_v, xt_s
+
+        def copy_out(xt_v, xt_s):
             grouped = stage.tile([P, ROWS_PER_PARTITION, P, 4], BF16, align_bytes=64)
             grouped_words = grouped[:].bitcast(F32)
             nc.vector.tensor_copy(out=grouped_words[:, 0:2, :, :], in_=xt_v[:].rearrange("j r u p -> j r p u"))
             nc.scalar.copy(out=grouped_words[:, 2:4, :, :], in_=xt_s[:].rearrange("j r u p -> j r p u"))
+            return grouped
+
+        def quantise(grouped):
             x_codes = stage.tile([P, GROUP_ROWS], U32, align_bytes=64)
             x_plane = stage.tile([P, GROUP_ROWS], U8, align_bytes=64)
             nc.vector.quantize_mx(
@@ -157,88 +168,110 @@ def tile_linearnnencoder_kernel(tc, x, W_words, W_scales, b, out):
             )
             return x_codes, x_plane
 
-        def consume(g, x_codes, x_plane):
-            for f in range(F_TILES):
-                z = psum_z.tile([P, GROUP_ROWS], F32)
-                nc.tensor.matmul_mx(
-                    out=z[:],
-                    rhs=x_codes[:].bitcast(FP8X4),
-                    rhs_scale=x_plane[:],
-                    start=True,
-                    stop=True,
-                    **w_tile(f),
+        def consume(g, f, x_codes, x_plane):
+            z = psum_z.tile([P, GROUP_ROWS], F32)
+            nc.tensor.matmul_mx(
+                out=z[:],
+                lhsT=w_codes[:, f * P * 4 : (f + 1) * P * 4].bitcast(FP8X4),
+                lhsT_scale=w_plane[:, f * P : (f + 1) * P],
+                rhs=x_codes[:].bitcast(FP8X4),
+                rhs_scale=x_plane[:],
+                start=True,
+                stop=True,
+            )
+            y = acts.tile([P, GROUP_ROWS], F32)
+            nc.scalar.activation(out=y[:], in_=z[:], func=ACT.Gelu, bias=bias[:, f : f + 1])
+            y_by_sample = y[:].rearrange("o (r s h) -> o r s h", r=ROWS_PER_PARTITION, s=GROUP_SAMPLES)
+            for pair in range(GROUP_SAMPLES // 2):
+                s = g * GROUP_SAMPLES + 2 * pair
+                nc.vector.bn_stats(
+                    out=stats[:, f, s : s + 2, :].rearrange("o e kind -> o (e kind)"),
+                    in_=y_by_sample[:, :, 2 * pair : 2 * pair + 2, :].rearrange("o r e h -> o r h e"),
                 )
-                y = acts.tile([P, GROUP_ROWS], F32)
-                nc.scalar.activation(out=y[:], in_=z[:], func=ACT.Gelu, bias=bias[:, f : f + 1])
-                y_by_sample = y[:].rearrange(
-                    "o (r s h) -> o r s h", r=ROWS_PER_PARTITION, s=GROUP_SAMPLES
-                )
-                for pair in range(GROUP_SAMPLES // 2):
-                    s = g * GROUP_SAMPLES + 2 * pair
-                    nc.vector.bn_stats(
-                        out=stats[:, f, s : s + 2, :].rearrange("o e kind -> o (e kind)"),
-                        in_=y_by_sample[:, :, 2 * pair : 2 * pair + 2, :].rearrange("o r e h -> o r h e"),
-                    )
-
-        ready = prepare(0)
-        for g in range(GROUPS):
-            current = ready
-            if g + 1 < GROUPS:
-                ready = prepare(g + 1)
-            consume(g, *current)
-
-        pad_y = const.tile([P, FEATURES], F32)
-        nc.scalar.activation(out=pad_y[:], in_=bias_everywhere[:], func=ACT.Gelu)
-
-        is_pad = const.tile([P, GROUPS, ROWS_PER_PARTITION], F32)
-        nc.vector.tensor_single_scalar(out=is_pad[:], in_=distance[:], scalar=0.0, op=ALU.is_equal)
-        pads_here = const.tile([P, GROUPS], F32)
-        nc.vector.tensor_reduce(out=pads_here[:], in_=is_pad[:], axis=AX.X, op=ALU.add)
-        spread = const.tile([P, GROUPS, GROUP_SAMPLES], BF16)
-        nc.vector.tensor_tensor(
-            out=spread[:],
-            in0=pads_here[:].unsqueeze(2).to_broadcast([P, GROUPS, GROUP_SAMPLES]),
-            in1=sample_of[:].unsqueeze(1).to_broadcast([P, GROUPS, GROUP_SAMPLES]),
-            op=ALU.mult,
-        )
-        pads_ps = psum_small.tile([P, 32], F32, tag="small")
-        nc.tensor.matmul(
-            out=pads_ps[:], lhsT=spread[:].rearrange("p g s -> p (g s)"), rhs=ones_bf[:], start=True, stop=True
-        )
 
         def column(name):
             return const.tile([P, 1], F32, name=name)
 
-        pads = column("pads")
-        nc.vector.tensor_copy(out=pads[:], in_=pads_ps[:, 0:1])
-        n = column("n")
-        nc.vector.tensor_scalar(out=n[:], in0=pads[:], scalar1=-1.0, scalar2=float(TOKENS), op0=ALU.mult, op1=ALU.add)
-        inv_n = column("inv_n")
-        nc.vector.tensor_scalar_max(out=inv_n[:], in0=n[:], scalar1=1.0)
-        nc.vector.reciprocal(out=inv_n[:], in_=inv_n[:])
-        some = column("some")
-        nc.vector.tensor_scalar_min(out=some[:], in0=n[:], scalar1=1.0)
-        nc.vector.tensor_mul(out=inv_n[:], in0=inv_n[:], in1=some[:])
         all_over_n = column("all_over_n")
-        nc.vector.tensor_scalar_mul(out=all_over_n[:], in0=inv_n[:], scalar1=float(TOKENS))
         pads_over_n = column("pads_over_n")
-        nc.vector.tensor_mul(out=pads_over_n[:], in0=pads[:], in1=inv_n[:])
         shift_weight = column("shift_weight")
-        nc.vector.tensor_scalar_mul(out=shift_weight[:], in0=pads_over_n[:], scalar1=float(TOKENS))
-        n_less_1 = column("n_less_1")
-        nc.vector.tensor_scalar(out=n_less_1[:], in0=n[:], scalar1=-1.0, scalar2=0.0, op0=ALU.add, op1=ALU.max)
-        inv_n_less_1 = column("inv_n_less_1")
-        nc.vector.tensor_scalar_max(out=inv_n_less_1[:], in0=n_less_1[:], scalar1=1.0)
-        nc.vector.reciprocal(out=inv_n_less_1[:], in_=inv_n_less_1[:])
-        several = column("several")
-        nc.vector.tensor_scalar_min(out=several[:], in0=n_less_1[:], scalar1=1.0)
-        nc.vector.tensor_mul(out=inv_n_less_1[:], in0=inv_n_less_1[:], in1=several[:])
+        inverse = const.tile([P, 2], F32)
+        pad_y = const.tile([P, FEATURES], F32)
+        pad_part = const.tile([P, FEATURES], F32)
+
+        def count_valid_rows():
+            nc.scalar.activation(out=pad_y[:], in_=bias_everywhere[:], func=ACT.Gelu)
+
+            is_valid = const.tile([P, GROUPS, ROWS_PER_PARTITION], F32)
+            nc.gpsimd.tensor_single_scalar(out=is_valid[:], in_=distance[:], scalar=0.0, op=ALU.is_gt)
+            valid_of_2 = const.tile([P, GROUPS, 2], F32)
+            nc.gpsimd.tensor_add(out=valid_of_2[:], in0=is_valid[:, :, 0:2], in1=is_valid[:, :, 2:4])
+            valid_here = const.tile([P, GROUPS, 1], F32)
+            nc.gpsimd.tensor_add(out=valid_here[:], in0=valid_of_2[:, :, 0:1], in1=valid_of_2[:, :, 1:2])
+            spread = const.tile([P, GROUPS, GROUP_SAMPLES], BF16)
+            nc.gpsimd.tensor_tensor(
+                out=spread[:],
+                in0=valid_here[:].to_broadcast([P, GROUPS, GROUP_SAMPLES]),
+                in1=sample_of[:].unsqueeze(1).to_broadcast([P, GROUPS, GROUP_SAMPLES]),
+                op=ALU.mult,
+            )
+            n_ps = psum_z.tile([P, 32], F32, tag="z")
+            nc.tensor.matmul(
+                out=n_ps[:], lhsT=spread[:].rearrange("p g s -> p (g s)"), rhs=ones_bf[:], start=True, stop=True
+            )
+            n_twice = const.tile([P, 2], F32)
+            nc.vector.tensor_copy(out=n_twice[:], in_=n_ps[:, 0:2])
+            divisors = const.tile([P, 2], F32)
+            nc.gpsimd.tensor_sub(out=divisors[:], in0=n_twice[:], in1=zero_and_one[:])
+            positive = const.tile([P, 2], F32)
+            nc.gpsimd.tensor_scalar(
+                out=positive[:], in0=divisors[:], scalar1=1.0, scalar2=0.0, op0=ALU.min, op1=ALU.max
+            )
+            nc.gpsimd.tensor_scalar_max(out=divisors[:], in0=divisors[:], scalar1=1.0)
+            nc.gpsimd.tensor_tensor(out=inverse[:], in0=divisors[:], in1=minus_ones[:], op=ALU.pow)
+            nc.gpsimd.tensor_mul(out=inverse[:], in0=inverse[:], in1=positive[:])
+            nc.gpsimd.tensor_scalar_mul(out=all_over_n[:], in0=inverse[:, 0:1], scalar1=float(TOKENS))
+            nc.gpsimd.tensor_sub(out=pads_over_n[:], in0=all_over_n[:], in1=positive[:, 0:1])
+            nc.gpsimd.tensor_scalar_mul(out=shift_weight[:], in0=pads_over_n[:], scalar1=float(TOKENS))
+            nc.gpsimd.tensor_scalar(
+                out=pad_part[:], in0=pad_y[:], scalar1=pads_over_n[:], scalar2=1.0, op0=ALU.mult, op1=ALU.mult
+            )
+
+        transposed = {}
+        regrouped = {}
+        quantised = {}
+        test_padding(0)
+        transposed[0] = transpose_rows(0, keep_valid_rows(0))
+        test_padding(1)
+        transposed[1] = transpose_rows(1, keep_valid_rows(1))
+        regrouped[0] = copy_out(*transposed[0])
+        quantised[0] = quantise(regrouped[0])
+        test_padding(2)
+        transposed[2] = transpose_rows(2, keep_valid_rows(2))
+        regrouped[1] = copy_out(*transposed[1])
+        test_padding(3)
+        for i in range(GROUPS):
+            if i + 1 < GROUPS:
+                quantised[i + 1] = quantise(regrouped[i + 1])
+            if i + 3 < GROUPS:
+                keep_rows = keep_valid_rows(i + 3)
+            consume(i, 0, *quantised[i])
+            consume(i, 1, *quantised[i])
+            if i + 2 < GROUPS:
+                regrouped[i + 2] = copy_out(*transposed[i + 2])
+            consume(i, 2, *quantised[i])
+            consume(i, 3, *quantised[i])
+            if i + 3 < GROUPS:
+                transposed[i + 3] = transpose_rows(i + 3, keep_rows)
+            if i + 4 < GROUPS:
+                test_padding(i + 4)
+            if i + 4 == GROUPS:
+                count_valid_rows()
 
         mean_all = psum_x.tile([P, F_TILES, P], F32, tag="xt_v")
         m2_all = psum_x.tile([P, F_TILES, P], F32, tag="xt_s")
         for f in range(F_TILES):
             nc.tensor.transpose(mean_all[:, f, :], stats[:, f, :, 1], ident[:])
-        for f in range(F_TILES):
             nc.tensor.transpose(m2_all[:, f, :], stats[:, f, :, 2], ident[:])
         mean_all_flat = mean_all[:].rearrange("s f o -> s (f o)")
         m2_all_flat = m2_all[:].rearrange("s f o -> s (f o)")
@@ -254,11 +287,9 @@ def tile_linearnnencoder_kernel(tc, x, W_words, W_scales, b, out):
         m2_valid = const.tile([P, FEATURES], F32)
         nc.vector.tensor_tensor(out=m2_valid[:], in0=m2_all_flat, in1=shift[:], op=ALU.subtract)
         nc.vector.tensor_scalar_max(out=m2_valid[:], in0=m2_valid[:], scalar1=0.0)
-        nc.scalar.activation(out=result[:, 0:FEATURES], in_=m2_valid[:], func=ACT.Sqrt, scale=inv_n_less_1[:])
+        nc.scalar.activation(out=result[:, 0:FEATURES], in_=m2_valid[:], func=ACT.Sqrt, scale=inverse[:, 1:2])
         nc.sync.dma_start(out=out[:, 0:FEATURES], in_=result[:, 0:FEATURES])
 
-        pad_part = const.tile([P, FEATURES], F32)
-        nc.vector.tensor_scalar_mul(out=pad_part[:], in0=pad_y[:], scalar1=pads_over_n[:])
         nc.vector.scalar_tensor_tensor(
             out=result[:, FEATURES : 2 * FEATURES],
             in0=mean_all_flat,

@@ -42,7 +42,6 @@ def tile_linearnnencoder_kernel(tc, x, W_words, W_scales, b, out):
         acts = scopes.enter_context(tc.tile_pool(name="acts", bufs=4))
         psum_x = scopes.enter_context(tc.psum_pool(name="psum_x", bufs=2))
         psum_z = scopes.enter_context(tc.psum_pool(name="psum_z", bufs=4))
-        scopes.enter_context(tc.manual_schedule())
 
         zero_col = const.tile([P, 1], F32)
         nc.vector.memset(zero_col[:], 0.0)

@@ -55,12 +55,11 @@ def tile_linearnnencoder_kernel(tc, x, W_words, W_scales, b, out):
         x_all = const.tile([P, GROUPS, ROWS_PER_PARTITION * K], BF16)
 
         def load_x(g):
-            nc.sync.dma_start(
-                out=x_all[:, g, :],
-                in_=rows[g * GROUP_ROWS : (g + 1) * GROUP_ROWS, :].rearrange(
-                    "(p r) k -> p (r k)", r=ROWS_PER_PARTITION
-                ),
+            group = rows[g * GROUP_ROWS : (g + 1) * GROUP_ROWS, :].rearrange(
+                "(p r) k -> p (r k)", r=ROWS_PER_PARTITION
             )
+            for half in (slice(0, 2 * K), slice(2 * K, 4 * K)):
+                nc.sync.dma_start(out=x_all[:, g, half], in_=group[:, half])
 
         load_x(0)
         load_x(1)
@@ -236,33 +235,28 @@ def tile_linearnnencoder_kernel(tc, x, W_words, W_scales, b, out):
                 out=pad_part[:], in0=pad_y[:], scalar1=pads_over_n[:], scalar2=1.0, op0=ALU.mult, op1=ALU.mult
             )
 
+        def live(g):
+            return 0 <= g < GROUPS
+
         transposed = {}
         regrouped = {}
         quantised = {}
-        test_padding(0)
-        transposed[0] = transpose_rows(0, keep_valid_rows(0))
-        test_padding(1)
-        transposed[1] = transpose_rows(1, keep_valid_rows(1))
-        regrouped[0] = copy_out(*transposed[0])
-        quantised[0] = quantise(regrouped[0])
-        test_padding(2)
-        transposed[2] = transpose_rows(2, keep_valid_rows(2))
-        regrouped[1] = copy_out(*transposed[1])
-        test_padding(3)
-        for i in range(GROUPS):
-            if i + 1 < GROUPS:
+        for i in range(-4, GROUPS):
+            if live(i + 1):
                 quantised[i + 1] = quantise(regrouped[i + 1])
-            if i + 3 < GROUPS:
+            if live(i + 3):
                 keep_rows = keep_valid_rows(i + 3)
-            consume(i, 0, *quantised[i])
-            consume(i, 1, *quantised[i])
-            if i + 2 < GROUPS:
+            if live(i):
+                for f in range(0, F_TILES // 2):
+                    consume(i, f, *quantised[i])
+            if live(i + 2):
                 regrouped[i + 2] = copy_out(*transposed[i + 2])
-            consume(i, 2, *quantised[i])
-            consume(i, 3, *quantised[i])
-            if i + 3 < GROUPS:
+            if live(i):
+                for f in range(F_TILES // 2, F_TILES):
+                    consume(i, f, *quantised[i])
+            if live(i + 3):
                 transposed[i + 3] = transpose_rows(i + 3, keep_rows)
-            if i + 4 < GROUPS:
+            if live(i + 4):
                 test_padding(i + 4)
             if i + 4 == GROUPS:
                 count_valid_rows()
@@ -278,16 +272,21 @@ def tile_linearnnencoder_kernel(tc, x, W_words, W_scales, b, out):
         result = const.tile([P, 2 * FEATURES], F32)
 
         gap = const.tile([P, FEATURES], F32)
-        nc.vector.tensor_tensor(out=gap[:], in0=mean_all_flat, in1=pad_y[:], op=ALU.subtract)
         shift = const.tile([P, FEATURES], F32)
-        nc.vector.scalar_tensor_tensor(
-            out=shift[:], in0=gap[:], scalar=shift_weight[:], in1=gap[:], op0=ALU.mult, op1=ALU.mult
-        )
         m2_valid = const.tile([P, FEATURES], F32)
-        nc.vector.tensor_tensor(out=m2_valid[:], in0=m2_all_flat, in1=shift[:], op=ALU.subtract)
-        nc.vector.tensor_scalar_max(out=m2_valid[:], in0=m2_valid[:], scalar1=0.0)
-        nc.scalar.activation(out=result[:, 0:FEATURES], in_=m2_valid[:], func=ACT.Sqrt, scale=inverse[:, 1:2])
-        nc.sync.dma_start(out=out[:, 0:FEATURES], in_=result[:, 0:FEATURES])
+        halves = (slice(0, FEATURES // 2), slice(FEATURES // 2, FEATURES))
+        for h in halves:
+            nc.vector.tensor_tensor(out=gap[:, h], in0=mean_all_flat[:, h], in1=pad_y[:, h], op=ALU.subtract)
+        for h in halves:
+            nc.vector.scalar_tensor_tensor(
+                out=shift[:, h], in0=gap[:, h], scalar=shift_weight[:], in1=gap[:, h], op0=ALU.mult, op1=ALU.mult
+            )
+        for h in halves:
+            nc.vector.tensor_tensor(out=m2_valid[:, h], in0=m2_all_flat[:, h], in1=shift[:, h], op=ALU.subtract)
+        for h in halves:
+            nc.vector.tensor_scalar_max(out=m2_valid[:, h], in0=m2_valid[:, h], scalar1=0.0)
+            nc.scalar.activation(out=result[:, h], in_=m2_valid[:, h], func=ACT.Sqrt, scale=inverse[:, 1:2])
+            nc.sync.dma_start(out=out[:, h], in_=result[:, h])
 
         nc.vector.scalar_tensor_tensor(
             out=result[:, FEATURES : 2 * FEATURES],

@@ -149,10 +149,13 @@ def tile_linearnnencoder_kernel(tc, x, W_words, W_scales, b, out):
                     )
             return xt_v, xt_s
 
-        def copy_out(xt_v, xt_s):
+        def copy_out(g, xt_v, xt_s):
             grouped = stage.tile([P, ROWS_PER_PARTITION, P, 4], BF16, align_bytes=64)
             grouped_words = grouped[:].bitcast(F32)
-            nc.vector.tensor_copy(out=grouped_words[:, 0:2, :, :], in_=xt_v[:].rearrange("j r u p -> j r p u"))
+            if g % 3 == 1:
+                nc.scalar.copy(out=grouped_words[:, 0:2, :, :], in_=xt_v[:].rearrange("j r u p -> j r p u"))
+            else:
+                nc.vector.tensor_copy(out=grouped_words[:, 0:2, :, :], in_=xt_v[:].rearrange("j r u p -> j r p u"))
             nc.scalar.copy(out=grouped_words[:, 2:4, :, :], in_=xt_s[:].rearrange("j r u p -> j r p u"))
             return grouped
 
@@ -250,7 +253,7 @@ def tile_linearnnencoder_kernel(tc, x, W_words, W_scales, b, out):
                 for f in range(0, F_TILES // 2):
                     consume(i, f, *quantised[i])
             if live(i + 2):
-                regrouped[i + 2] = copy_out(*transposed[i + 2])
+                regrouped[i + 2] = copy_out(i + 2, *transposed[i + 2])
             if live(i):
                 for f in range(F_TILES // 2, F_TILES):
                     consume(i, f, *quantised[i])

@@ -39,7 +39,7 @@ def tile_linearnnencoder_kernel(tc, x, W_words, W_scales, b, out):
     with ExitStack() as scopes:
         const = scopes.enter_context(tc.tile_pool(name="const", bufs=1))
         stage = scopes.enter_context(tc.tile_pool(name="stage", bufs=3))
-        acts = scopes.enter_context(tc.tile_pool(name="acts", bufs=4))
+        acts = scopes.enter_context(tc.tile_pool(name="acts", bufs=8))
         psum_x = scopes.enter_context(tc.psum_pool(name="psum_x", bufs=2))
         psum_z = scopes.enter_context(tc.psum_pool(name="psum_z", bufs=4))
 
@@ -105,6 +105,13 @@ def tile_linearnnencoder_kernel(tc, x, W_words, W_scales, b, out):
         nc.tensor.transpose(bias_ps[:], bias_rows[:], ident[:])
         bias = const.tile([P, F_TILES], F32)
         nc.vector.tensor_copy(out=bias[:], in_=bias_ps[:, 0:F_TILES])
+
+        pad_y_column = const.tile([P, F_TILES], F32)
+        nc.scalar.activation(out=pad_y_column[:], in_=bias[:], func=ACT.Gelu)
+        minus_pad_y_block = const.tile([P, F_TILES, P], F32)
+        nc.vector.tensor_scalar_mul(
+            out=minus_pad_y_block[:], in0=pad_y_column[:].unsqueeze(2).to_broadcast([P, F_TILES, P]), scalar1=-1.0
+        )
 
         stats = const.tile([P, F_TILES, SAMPLES, 3], F32)
         distance = const.tile([P, GROUPS, ROWS_PER_PARTITION], F32)
@@ -189,16 +196,17 @@ def tile_linearnnencoder_kernel(tc, x, W_words, W_scales, b, out):
                     out=stats[:, f, s : s + 2, :].rearrange("o e kind -> o (e kind)"),
                     in_=y_by_sample[:, :, 2 * pair : 2 * pair + 2, :].rearrange("o r e h -> o r h e"),
                 )
+            return y
 
         def column(name):
             return const.tile([P, 1], F32, name=name)
 
         all_over_n = column("all_over_n")
         pads_over_n = column("pads_over_n")
-        shift_weight = column("shift_weight")
+        minus_shift_weight = column("minus_shift_weight")
         inverse = const.tile([P, 2], F32)
         pad_y = const.tile([P, FEATURES], F32)
-        pad_part = const.tile([P, FEATURES], F32)
+        pad_y_if_any = const.tile([P, FEATURES], F32)
 
         def count_valid_rows():
             nc.scalar.activation(out=pad_y[:], in_=bias_everywhere[:], func=ACT.Gelu)
@@ -233,9 +241,9 @@ def tile_linearnnencoder_kernel(tc, x, W_words, W_scales, b, out):
             nc.gpsimd.tensor_mul(out=inverse[:], in0=inverse[:], in1=positive[:])
             nc.gpsimd.tensor_scalar_mul(out=all_over_n[:], in0=inverse[:, 0:1], scalar1=float(TOKENS))
             nc.gpsimd.tensor_sub(out=pads_over_n[:], in0=all_over_n[:], in1=positive[:, 0:1])
-            nc.gpsimd.tensor_scalar_mul(out=shift_weight[:], in0=pads_over_n[:], scalar1=float(TOKENS))
+            nc.gpsimd.tensor_scalar_mul(out=minus_shift_weight[:], in0=pads_over_n[:], scalar1=-float(TOKENS))
             nc.gpsimd.tensor_scalar(
-                out=pad_part[:], in0=pad_y[:], scalar1=pads_over_n[:], scalar2=1.0, op0=ALU.mult, op1=ALU.mult
+                out=pad_y_if_any[:], in0=pad_y[:], scalar1=positive[:, 0:1], scalar2=1.0, op0=ALU.mult, op1=ALU.mult
             )
 
         def live(g):
@@ -256,7 +264,7 @@ def tile_linearnnencoder_kernel(tc, x, W_words, W_scales, b, out):
                 regrouped[i + 2] = copy_out(i + 2, *transposed[i + 2])
             if live(i):
                 for f in range(F_TILES // 2, F_TILES):
-                    consume(i, f, *quantised[i])
+                    last_y = consume(i, f, *quantised[i])
             if live(i + 3):
                 transposed[i + 3] = transpose_rows(i + 3, keep_rows)
             if live(i + 4):
@@ -264,39 +272,53 @@ def tile_linearnnencoder_kernel(tc, x, W_words, W_scales, b, out):
             if i + 4 == GROUPS:
                 count_valid_rows()
 
-        mean_all = psum_x.tile([P, F_TILES, P], F32, tag="xt_v")
+        nc.scalar.activation(out=warm_col[:], in_=last_y[:, 0:1], func=ACT.Sqrt, scale=0.0)
+
+        gap = psum_x.tile([P, F_TILES, P], F32, tag="xt_v")
         m2_all = psum_x.tile([P, F_TILES, P], F32, tag="xt_s")
         for f in range(F_TILES):
-            nc.tensor.transpose(mean_all[:, f, :], stats[:, f, :, 1], ident[:])
+            nc.tensor.matmul(
+                out=gap[:, f, :], lhsT=minus_pad_y_block[:, f, :], rhs=ident[:], is_transpose=True, start=f == 0, stop=False
+            )
+        for f in range(F_TILES):
             nc.tensor.transpose(m2_all[:, f, :], stats[:, f, :, 2], ident[:])
-        mean_all_flat = mean_all[:].rearrange("s f o -> s (f o)")
+            nc.tensor.matmul(
+                out=gap[:, f, :],
+                lhsT=stats[:, f, :, 1],
+                rhs=ident[:],
+                is_transpose=True,
+                start=False,
+                stop=f == F_TILES - 1,
+            )
+        gap_flat = gap[:].rearrange("s f o -> s (f o)")
         m2_all_flat = m2_all[:].rearrange("s f o -> s (f o)")
 
         result = const.tile([P, 2 * FEATURES], F32)
 
-        gap = const.tile([P, FEATURES], F32)
-        shift = const.tile([P, FEATURES], F32)
+        gap_squared = const.tile([P, FEATURES], F32)
         m2_valid = const.tile([P, FEATURES], F32)
         halves = (slice(0, FEATURES // 2), slice(FEATURES // 2, FEATURES))
         for h in halves:
-            nc.vector.tensor_tensor(out=gap[:, h], in0=mean_all_flat[:, h], in1=pad_y[:, h], op=ALU.subtract)
+            nc.scalar.activation(out=gap_squared[:, h], in_=gap_flat[:, h], func=ACT.Square)
         for h in halves:
             nc.vector.scalar_tensor_tensor(
-                out=shift[:, h], in0=gap[:, h], scalar=shift_weight[:], in1=gap[:, h], op0=ALU.mult, op1=ALU.mult
+                out=m2_valid[:, h],
+                in0=gap_squared[:, h],
+                scalar=minus_shift_weight[:],
+                in1=m2_all_flat[:, h],
+                op0=ALU.mult,
+                op1=ALU.add,
             )
-        for h in halves:
-            nc.vector.tensor_tensor(out=m2_valid[:, h], in0=m2_all_flat[:, h], in1=shift[:, h], op=ALU.subtract)
-        for h in halves:
             nc.vector.tensor_scalar_max(out=m2_valid[:, h], in0=m2_valid[:, h], scalar1=0.0)
             nc.scalar.activation(out=result[:, h], in_=m2_valid[:, h], func=ACT.Sqrt, scale=inverse[:, 1:2])
             nc.sync.dma_start(out=out[:, h], in_=result[:, h])
 
         nc.vector.scalar_tensor_tensor(
             out=result[:, FEATURES : 2 * FEATURES],
-            in0=mean_all_flat,
+            in0=gap_flat,
             scalar=all_over_n[:],
-            in1=pad_part[:],
+            in1=pad_y_if_any[:],
             op0=ALU.mult,
-            op1=ALU.subtract,
+            op1=ALU.add,
         )
         nc.sync.dma_start(out=out[:, FEATURES : 2 * FEATURES], in_=result[:, FEATURES : 2 * FEATURES])

@@ -178,15 +178,16 @@ def tile_linearnnencoder_kernel(tc, x, W_words, W_scales, b, out):
 
         def consume(g, f, x_codes, x_plane):
             z = psum_z.tile([P, GROUP_ROWS], F32)
-            nc.tensor.matmul_mx(
-                out=z[:],
-                lhsT=w_codes[:, f * P * 4 : (f + 1) * P * 4].bitcast(FP8X4),
-                lhsT_scale=w_plane[:, f * P : (f + 1) * P],
-                rhs=x_codes[:].bitcast(FP8X4),
-                rhs_scale=x_plane[:],
-                start=True,
-                stop=True,
-            )
+            for repeat in range(2):
+                nc.tensor.matmul_mx(
+                    out=z[:],
+                    lhsT=w_codes[:, f * P * 4 : (f + 1) * P * 4].bitcast(FP8X4),
+                    lhsT_scale=w_plane[:, f * P : (f + 1) * P],
+                    rhs=x_codes[:].bitcast(FP8X4),
+                    rhs_scale=x_plane[:],
+                    start=True,
+                    stop=True,
+                )
             y = acts.tile([P, GROUP_ROWS], F32)
             nc.scalar.activation(out=y[:], in_=z[:], func=ACT.Gelu, bias=bias[:, f : f + 1])
             y_by_sample = y[:].rearrange("o (r s h) -> o r s h", r=ROWS_PER_PARTITION, s=GROUP_SAMPLES)

@@ -159,7 +159,7 @@ def tile_linearnnencoder_kernel(tc, x, W_words, W_scales, b, out):
         def copy_out(g, xt_v, xt_s):
             grouped = stage.tile([P, ROWS_PER_PARTITION, P, 4], BF16, align_bytes=64)
             grouped_words = grouped[:].bitcast(F32)
-            if g % 3 == 1:
+            if g >= GROUPS - 3:
                 nc.scalar.copy(out=grouped_words[:, 0:2, :, :], in_=xt_v[:].rearrange("j r u p -> j r p u"))
             else:
                 nc.vector.tensor_copy(out=grouped_words[:, 0:2, :, :], in_=xt_v[:].rearrange("j r u p -> j r p u"))

@@ -31,6 +31,17 @@ PAD_WORD = -(1.0 + 0xBF80 / 2.0**23)
 
 FLOPS = 2 * SAMPLES * TOKENS * K * FEATURES
 
+VECTOR_TEST_GROUPS = 4
+VECTOR_COPY_GROUPS = 5
+WARM_UP_MATMULS = 4
+HOLD_MATMULS = 2
+
+LEAD_TEST = 12
+LEAD_KEEP = 11
+LEAD_TRANSPOSE = 7
+LEAD_COPY = 6
+LEAD_QUANTISE = 5
+
 
 def tile_linearnnencoder_kernel(tc, x, W_words, W_scales, b, out):
     nc = tc.nc
@@ -42,15 +53,7 @@ def tile_linearnnencoder_kernel(tc, x, W_words, W_scales, b, out):
         acts = scopes.enter_context(tc.tile_pool(name="acts", bufs=8))
         psum_x = scopes.enter_context(tc.psum_pool(name="psum_x", bufs=2))
         psum_z = scopes.enter_context(tc.psum_pool(name="psum_z", bufs=4))
-
-        zero_col = const.tile([P, 1], F32)
-        nc.vector.memset(zero_col[:], 0.0)
-        warm_col = const.tile([P, 1], F32)
-        nc.scalar.activation(out=warm_col[:], in_=zero_col[:], func=ACT.Gelu)
-
-        bias_rows_bf = const.tile([P, P], BF16)
-        nc.vector.memset(bias_rows_bf[:], 0.0)
-        nc.sync.dma_start(out=bias_rows_bf[0:F_TILES, :], in_=b.rearrange("(f c) -> f c", f=F_TILES))
+        scopes.enter_context(tc.manual_schedule())
 
         x_all = const.tile([P, GROUPS, ROWS_PER_PARTITION * K], BF16)
 
@@ -61,15 +64,25 @@ def tile_linearnnencoder_kernel(tc, x, W_words, W_scales, b, out):
             for half in (slice(0, 2 * K), slice(2 * K, 4 * K)):
                 nc.sync.dma_start(out=x_all[:, g, half], in_=group[:, half])
 
+        bias_rows_bf = const.tile([P, P], BF16)
+        ones_bf = const.tile([P, GROUP_ROWS], BF16)
+        zero_col = const.tile([P, 1], F32)
+        w_plane = const.tile([P, FEATURES], U8, align_bytes=64)
+        minus_pad_word = const.tile([P, 1], F32)
+        nc.vector.memset(zero_col[:], 0.0)
+        nc.vector.memset(ones_bf[:], 1.0)
+        nc.vector.memset(minus_pad_word[:], -PAD_WORD)
+        nc.vector.memset(bias_rows_bf[:], 0.0)
+        nc.vector.memset(w_plane[:].bitcast(I32), 0)
+
         load_x(0)
+        nc.sync.dma_start(out=bias_rows_bf[0:F_TILES, :], in_=b.rearrange("(f c) -> f c", f=F_TILES))
         load_x(1)
         w_codes = const.tile([P, FEATURES * 4], U8, align_bytes=64)
         nc.sync.dma_start(
             out=w_codes[:].bitcast(I32),
             in_=W_words.rearrange("o p n t -> p (o n t)").bitcast(I32),
         )
-        w_plane = const.tile([P, FEATURES], U8, align_bytes=64)
-        nc.vector.memset(w_plane[:].bitcast(I32), 0)
         for quadrant in range(4):
             nc.sync.dma_start(
                 out=w_plane[32 * quadrant : 32 * quadrant + 4, :].bitcast(I32),
@@ -80,38 +93,32 @@ def tile_linearnnencoder_kernel(tc, x, W_words, W_scales, b, out):
         bias_everywhere = const.tile([P, FEATURES], BF16)
         nc.sync.dma_start(out=bias_everywhere[:], in_=b.partition_broadcast(P))
 
+        warm_col = const.tile([P, 1], F32)
+        nc.scalar.activation(out=warm_col[:], in_=zero_col[:], func=ACT.Gelu)
+
         ident = const.tile([P, P], F32)
         make_identity(nc, ident[:])
-        minus_pad_word = const.tile([P, 1], F32)
-        nc.vector.memset(minus_pad_word[:], -PAD_WORD)
-        ones_bf = const.tile([P, 32], BF16)
-        nc.vector.memset(ones_bf[:], 1.0)
         minus_ones = const.tile([P, 2], F32)
-        nc.vector.memset(minus_ones[:], -1.0)
+        nc.gpsimd.memset(minus_ones[:], -1.0)
         zero_and_one = const.tile([P, 2], F32)
-        nc.vector.memset(zero_and_one[:, 0:1], 0.0)
-        nc.vector.memset(zero_and_one[:, 1:2], 1.0)
-        sample_of = const.tile([P, GROUP_SAMPLES], F32)
-        nc.vector.tensor_reduce(
-            out=sample_of[:],
-            in_=ident[:].rearrange("p (s h) -> p s h", h=PARTITIONS_PER_SAMPLE),
-            axis=AX.X,
-            op=ALU.add,
-        )
+        nc.gpsimd.memset(zero_and_one[:, 0:1], 0.0)
+        nc.gpsimd.memset(zero_and_one[:, 1:2], 1.0)
+
+        def unread_matmuls(count):
+            unread = psum_z.tile([P, GROUP_ROWS], F32, tag="z")
+            for repeat in range(count):
+                nc.tensor.matmul(out=unread[:], lhsT=ones_bf[:, 0:P], rhs=ones_bf[:], start=True, stop=True)
+
+        unread_matmuls(WARM_UP_MATMULS)
 
         bias_rows = const.tile([P, P], F32)
-        nc.vector.tensor_copy(out=bias_rows[:], in_=bias_rows_bf[:])
-        bias_ps = psum_z.tile([P, P], F32, tag="z")
-        nc.tensor.transpose(bias_ps[:], bias_rows[:], ident[:])
         bias = const.tile([P, F_TILES], F32)
-        nc.vector.tensor_copy(out=bias[:], in_=bias_ps[:, 0:F_TILES])
+        sample_of = const.tile([P, GROUP_SAMPLES], F32)
 
-        pad_y_column = const.tile([P, F_TILES], F32)
-        nc.scalar.activation(out=pad_y_column[:], in_=bias[:], func=ACT.Gelu)
-        minus_pad_y_block = const.tile([P, F_TILES, P], F32)
-        nc.vector.tensor_scalar_mul(
-            out=minus_pad_y_block[:], in0=pad_y_column[:].unsqueeze(2).to_broadcast([P, F_TILES, P]), scalar1=-1.0
-        )
+        def spread_bias():
+            bias_ps = psum_z.tile([P, P], F32, tag="z")
+            nc.tensor.transpose(bias_ps[:], bias_rows[:], ident[:])
+            return bias_ps
 
         stats = const.tile([P, F_TILES, SAMPLES, 3], F32)
         distance = const.tile([P, GROUPS, ROWS_PER_PARTITION], F32)
@@ -119,20 +126,31 @@ def tile_linearnnencoder_kernel(tc, x, W_words, W_scales, b, out):
         def x_words(g):
             return x_all[:, g, :].bitcast(F32)
 
-        def test_padding(g):
-            for r in range(ROWS_PER_PARTITION):
+        def test_row(g, r):
+            words = x_words(g)[:, r * WORDS : (r + 1) * WORDS]
+            if g < VECTOR_TEST_GROUPS and r % 2 == 1:
+                unlike = acts.tile([P, WORDS], BF16)
+                nc.vector.tensor_scalar(
+                    out=unlike[:],
+                    in0=words,
+                    scalar1=PAD_WORD,
+                    scalar2=0.0,
+                    op0=ALU.not_equal,
+                    op1=ALU.add,
+                    accum_out=distance[:, g, r : r + 1],
+                )
+            else:
                 squares = acts.tile([P, WORDS], BF16)
                 nc.scalar.activation(
                     out=squares[:],
-                    in_=x_words(g)[:, r * WORDS : (r + 1) * WORDS],
+                    in_=words,
                     func=ACT.Square,
                     bias=minus_pad_word[:],
                     accum_out=distance[:, g, r : r + 1],
                 )
 
-        def keep_valid_rows(g):
-            keep_rows = stage.tile([P, ROWS_PER_PARTITION, P], F32, bufs=2)
-            for r in range(ROWS_PER_PARTITION):
+        def keep_valid_rows(g, keep_rows, of_rows):
+            for r in of_rows:
                 nc.vector.tensor_scalar(
                     out=keep_rows[:, r, :],
                     in0=ident[:],
@@ -141,7 +159,6 @@ def tile_linearnnencoder_kernel(tc, x, W_words, W_scales, b, out):
                     op0=ALU.mult,
                     op1=ALU.is_gt,
                 )
-            return keep_rows
 
         def transpose_rows(g, keep_rows):
             xt_v = psum_x.tile([P, 2, 2, P], F32)
@@ -156,13 +173,13 @@ def tile_linearnnencoder_kernel(tc, x, W_words, W_scales, b, out):
                     )
             return xt_v, xt_s
 
-        def copy_out(g, xt_v, xt_s):
+        def regroup(g, xt_v, xt_s):
             grouped = stage.tile([P, ROWS_PER_PARTITION, P, 4], BF16, align_bytes=64)
             grouped_words = grouped[:].bitcast(F32)
-            if g >= GROUPS - 3:
-                nc.scalar.copy(out=grouped_words[:, 0:2, :, :], in_=xt_v[:].rearrange("j r u p -> j r p u"))
-            else:
+            if g < VECTOR_COPY_GROUPS:
                 nc.vector.tensor_copy(out=grouped_words[:, 0:2, :, :], in_=xt_v[:].rearrange("j r u p -> j r p u"))
+            else:
+                nc.scalar.copy(out=grouped_words[:, 0:2, :, :], in_=xt_v[:].rearrange("j r u p -> j r p u"))
             nc.scalar.copy(out=grouped_words[:, 2:4, :, :], in_=xt_s[:].rearrange("j r u p -> j r p u"))
             return grouped
 
@@ -176,9 +193,9 @@ def tile_linearnnencoder_kernel(tc, x, W_words, W_scales, b, out):
             )
             return x_codes, x_plane
 
-        def consume(g, f, x_codes, x_plane):
+        def multiply(g, f, x_codes, x_plane):
             z = psum_z.tile([P, GROUP_ROWS], F32)
-            for repeat in range(2):
+            for repeat in range(1 if g == 0 and f == 0 else 2):
                 nc.tensor.matmul_mx(
                     out=z[:],
                     lhsT=w_codes[:, f * P * 4 : (f + 1) * P * 4].bitcast(FP8X4),
@@ -188,8 +205,14 @@ def tile_linearnnencoder_kernel(tc, x, W_words, W_scales, b, out):
                     start=True,
                     stop=True,
                 )
+            return z
+
+        def gelu(f, z):
             y = acts.tile([P, GROUP_ROWS], F32)
             nc.scalar.activation(out=y[:], in_=z[:], func=ACT.Gelu, bias=bias[:, f : f + 1])
+            return y
+
+        def statistics(g, f, y):
             y_by_sample = y[:].rearrange("o (r s h) -> o r s h", r=ROWS_PER_PARTITION, s=GROUP_SAMPLES)
             for pair in range(GROUP_SAMPLES // 2):
                 s = g * GROUP_SAMPLES + 2 * pair
@@ -197,7 +220,6 @@ def tile_linearnnencoder_kernel(tc, x, W_words, W_scales, b, out):
                     out=stats[:, f, s : s + 2, :].rearrange("o e kind -> o (e kind)"),
                     in_=y_by_sample[:, :, 2 * pair : 2 * pair + 2, :].rearrange("o r e h -> o r h e"),
                 )
-            return y
 
         def column(name):
             return const.tile([P, 1], F32, name=name)
@@ -205,35 +227,39 @@ def tile_linearnnencoder_kernel(tc, x, W_words, W_scales, b, out):
         all_over_n = column("all_over_n")
         pads_over_n = column("pads_over_n")
         minus_shift_weight = column("minus_shift_weight")
+        positive = const.tile([P, 2], F32)
         inverse = const.tile([P, 2], F32)
         pad_y = const.tile([P, FEATURES], F32)
         pad_y_if_any = const.tile([P, FEATURES], F32)
+        minus_pad_y_column = const.tile([P, F_TILES], F32)
+        spread = const.tile([P, GROUPS, GROUP_SAMPLES], BF16)
 
-        def count_valid_rows():
-            nc.scalar.activation(out=pad_y[:], in_=bias_everywhere[:], func=ACT.Gelu)
-
+        def spread_counts():
             is_valid = const.tile([P, GROUPS, ROWS_PER_PARTITION], F32)
             nc.gpsimd.tensor_single_scalar(out=is_valid[:], in_=distance[:], scalar=0.0, op=ALU.is_gt)
             valid_of_2 = const.tile([P, GROUPS, 2], F32)
             nc.gpsimd.tensor_add(out=valid_of_2[:], in0=is_valid[:, :, 0:2], in1=is_valid[:, :, 2:4])
             valid_here = const.tile([P, GROUPS, 1], F32)
             nc.gpsimd.tensor_add(out=valid_here[:], in0=valid_of_2[:, :, 0:1], in1=valid_of_2[:, :, 1:2])
-            spread = const.tile([P, GROUPS, GROUP_SAMPLES], BF16)
             nc.gpsimd.tensor_tensor(
                 out=spread[:],
                 in0=valid_here[:].to_broadcast([P, GROUPS, GROUP_SAMPLES]),
                 in1=sample_of[:].unsqueeze(1).to_broadcast([P, GROUPS, GROUP_SAMPLES]),
                 op=ALU.mult,
             )
+
+        def count_valid_rows():
             n_ps = psum_z.tile([P, 32], F32, tag="z")
             nc.tensor.matmul(
-                out=n_ps[:], lhsT=spread[:].rearrange("p g s -> p (g s)"), rhs=ones_bf[:], start=True, stop=True
+                out=n_ps[:], lhsT=spread[:].rearrange("p g s -> p (g s)"), rhs=ones_bf[:, 0:32], start=True, stop=True
             )
+            return n_ps
+
+        def weights_of_samples(n_ps):
             n_twice = const.tile([P, 2], F32)
             nc.vector.tensor_copy(out=n_twice[:], in_=n_ps[:, 0:2])
             divisors = const.tile([P, 2], F32)
             nc.gpsimd.tensor_sub(out=divisors[:], in0=n_twice[:], in1=zero_and_one[:])
-            positive = const.tile([P, 2], F32)
             nc.gpsimd.tensor_scalar(
                 out=positive[:], in0=divisors[:], scalar1=1.0, scalar2=0.0, op0=ALU.min, op1=ALU.max
             )
@@ -243,83 +269,143 @@ def tile_linearnnencoder_kernel(tc, x, W_words, W_scales, b, out):
             nc.gpsimd.tensor_scalar_mul(out=all_over_n[:], in0=inverse[:, 0:1], scalar1=float(TOKENS))
             nc.gpsimd.tensor_sub(out=pads_over_n[:], in0=all_over_n[:], in1=positive[:, 0:1])
             nc.gpsimd.tensor_scalar_mul(out=minus_shift_weight[:], in0=pads_over_n[:], scalar1=-float(TOKENS))
+
+        def gelu_of_padding():
+            nc.scalar.activation(out=pad_y[:], in_=bias_everywhere[:], func=ACT.Gelu)
+            pad_y_column = const.tile([P, F_TILES], F32)
+            nc.scalar.activation(out=pad_y_column[:], in_=bias[:], func=ACT.Gelu)
             nc.gpsimd.tensor_scalar(
-                out=pad_y_if_any[:], in0=pad_y[:], scalar1=positive[:, 0:1], scalar2=1.0, op0=ALU.mult, op1=ALU.mult
+                out=minus_pad_y_column[:], in0=pad_y_column[:], scalar1=-1.0, scalar2=1.0, op0=ALU.mult, op1=ALU.mult
             )
 
-        def live(g):
-            return 0 <= g < GROUPS
-
-        transposed = {}
-        regrouped = {}
+        keep = {}
+        banks = {}
+        grouped = {}
         quantised = {}
-        for i in range(-4, GROUPS):
-            if live(i + 1):
-                quantised[i + 1] = quantise(regrouped[i + 1])
-            if live(i + 3):
-                keep_rows = keep_valid_rows(i + 3)
-            if live(i):
-                for f in range(0, F_TILES // 2):
-                    consume(i, f, *quantised[i])
-            if live(i + 2):
-                regrouped[i + 2] = copy_out(i + 2, *transposed[i + 2])
-            if live(i):
-                for f in range(F_TILES // 2, F_TILES):
-                    last_y = consume(i, f, *quantised[i])
-            if live(i + 3):
-                transposed[i + 3] = transpose_rows(i + 3, keep_rows)
-            if live(i + 4):
-                test_padding(i + 4)
-            if i + 4 == GROUPS:
-                count_valid_rows()
+        nc.vector.tensor_reduce(
+            out=sample_of[:],
+            in_=ident[:].rearrange("p (s h) -> p s h", h=PARTITIONS_PER_SAMPLE),
+            axis=AX.X,
+            op=ALU.add,
+        )
 
-        nc.scalar.activation(out=warm_col[:], in_=last_y[:, 0:1], func=ACT.Sqrt, scale=0.0)
+        def due(step, lead):
+            g, rest = divmod(step + lead, F_TILES)
+            return g if rest == 0 and 0 <= g < GROUPS else None
 
-        gap = psum_x.tile([P, F_TILES, P], F32, tag="xt_v")
-        m2_all = psum_x.tile([P, F_TILES, P], F32, tag="xt_s")
-        for f in range(F_TILES):
-            nc.tensor.matmul(
-                out=gap[:, f, :], lhsT=minus_pad_y_block[:, f, :], rhs=ident[:], is_transpose=True, start=f == 0, stop=False
-            )
-        for f in range(F_TILES):
-            nc.tensor.transpose(m2_all[:, f, :], stats[:, f, :, 2], ident[:])
-            nc.tensor.matmul(
-                out=gap[:, f, :],
-                lhsT=stats[:, f, :, 1],
-                rhs=ident[:],
-                is_transpose=True,
-                start=False,
-                stop=f == F_TILES - 1,
-            )
-        gap_flat = gap[:].rearrange("s f o -> s (f o)")
-        m2_all_flat = m2_all[:].rearrange("s f o -> s (f o)")
+        for n in range(-LEAD_TEST, F_TILES * GROUPS):
+            if n >= 0:
+                g, f = divmod(n, F_TILES)
+                y = gelu(f, multiply(g, f, *quantised[g]))
+                statistics(g, f, y)
+            g = due(n, LEAD_TEST)
+            if g is not None:
+                keep[g] = stage.tile([P, ROWS_PER_PARTITION, P], F32, name="keep_rows", bufs=2)
+                for half in ((0, 1), (2, 3)):
+                    for r in half:
+                        test_row(g, r)
+                    if g == 0:
+                        keep_valid_rows(g, keep[g], half)
+                if g == 0:
+                    nc.vector.tensor_copy(out=bias_rows[:], in_=bias_rows_bf[:])
+                if g == GROUPS - 1:
+                    spread_counts()
+            g = due(n, LEAD_KEEP)
+            if g is not None and g > 0:
+                keep_valid_rows(g, keep[g], range(ROWS_PER_PARTITION))
+            g = due(n, LEAD_TRANSPOSE)
+            if g is not None:
+                banks[g] = transpose_rows(g, keep[g])
+                if g == 0:
+                    unread_matmuls(HOLD_MATMULS)
+                    bias_ps = spread_bias()
+                if g == GROUPS - 1:
+                    n_ps = count_valid_rows()
+            g = due(n, LEAD_COPY)
+            if g is not None:
+                grouped[g] = regroup(g, *banks[g])
+            g = due(n, LEAD_QUANTISE)
+            if g is not None:
+                quantised[g] = quantise(grouped[g])
+                if g == 0:
+                    nc.vector.tensor_copy(out=bias[:], in_=bias_ps[:, 0:F_TILES])
+                if g == GROUPS - 1:
+                    weights_of_samples(n_ps)
+                    gelu_of_padding()
+                    nc.gpsimd.tensor_scalar(
+                        out=pad_y_if_any[:], in0=pad_y[:], scalar1=positive[:, 0:1], scalar2=1.0, op0=ALU.mult, op1=ALU.mult
+                    )
 
-        result = const.tile([P, 2 * FEATURES], F32)
+        nc.scalar.activation(out=warm_col[:], in_=y[:, 0:1], func=ACT.Sqrt, scale=0.0)
 
         gap_squared = const.tile([P, FEATURES], F32)
         m2_valid = const.tile([P, FEATURES], F32)
-        halves = (slice(0, FEATURES // 2), slice(FEATURES // 2, FEATURES))
-        for h in halves:
-            nc.scalar.activation(out=gap_squared[:, h], in_=gap_flat[:, h], func=ACT.Square)
-        for h in halves:
+        result = const.tile([P, 2 * FEATURES], F32)
+        parts = []
+        for first, last in ((0, F_TILES - 1), (F_TILES - 1, F_TILES)):
+            gap = psum_x.tile([P, F_TILES, P], F32, tag="xt_v")
+            m2_all = psum_x.tile([P, F_TILES, P], F32, tag="xt_s")
+            for f in range(first, last):
+                nc.tensor.matmul(
+                    out=gap[:, f, :],
+                    lhsT=minus_pad_y_column[:, f : f + 1].to_broadcast([P, P]),
+                    rhs=ident[:],
+                    is_transpose=True,
+                    start=f == first,
+                    stop=False,
+                )
+            for f in range(first, last):
+                nc.tensor.matmul(
+                    out=gap[:, f, :],
+                    lhsT=stats[:, f, :, 1],
+                    rhs=ident[:],
+                    is_transpose=True,
+                    start=False,
+                    stop=f == last - 1,
+                )
+            for f in range(first, last):
+                nc.tensor.transpose(m2_all[:, f, :], stats[:, f, :, 2], ident[:])
+            columns = slice(first * P, last * P)
+            parts.append(
+                (
+                    columns,
+                    slice(FEATURES + columns.start, FEATURES + columns.stop),
+                    gap[:].rearrange("s f o -> s (f o)")[:, columns],
+                    m2_all[:].rearrange("s f o -> s (f o)")[:, columns],
+                )
+            )
+
+        def mean_of(columns, mean_columns, gap_part, m2_part):
             nc.vector.scalar_tensor_tensor(
-                out=m2_valid[:, h],
-                in0=gap_squared[:, h],
-                scalar=minus_shift_weight[:],
-                in1=m2_all_flat[:, h],
+                out=result[:, mean_columns],
+                in0=gap_part,
+                scalar=all_over_n[:],
+                in1=pad_y_if_any[:, columns],
                 op0=ALU.mult,
                 op1=ALU.add,
             )
-            nc.vector.tensor_scalar_max(out=m2_valid[:, h], in0=m2_valid[:, h], scalar1=0.0)
-            nc.scalar.activation(out=result[:, h], in_=m2_valid[:, h], func=ACT.Sqrt, scale=inverse[:, 1:2])
-            nc.sync.dma_start(out=out[:, h], in_=result[:, h])
+            nc.sync.dma_start(out=out[:, mean_columns], in_=result[:, mean_columns])
 
-        nc.vector.scalar_tensor_tensor(
-            out=result[:, FEATURES : 2 * FEATURES],
-            in0=gap_flat,
-            scalar=all_over_n[:],
-            in1=pad_y_if_any[:],
-            op0=ALU.mult,
-            op1=ALU.add,
-        )
-        nc.sync.dma_start(out=out[:, FEATURES : 2 * FEATURES], in_=result[:, FEATURES : 2 * FEATURES])
+        def square_of(columns, mean_columns, gap_part, m2_part):
+            nc.scalar.activation(out=gap_squared[:, columns], in_=gap_part, func=ACT.Square)
+
+        def std_of(columns, mean_columns, gap_part, m2_part):
+            nc.vector.scalar_tensor_tensor(
+                out=m2_valid[:, columns],
+                in0=gap_squared[:, columns],
+                scalar=minus_shift_weight[:],
+                in1=m2_part,
+                op0=ALU.mult,
+                op1=ALU.add,
+            )
+            nc.vector.tensor_scalar_max(out=m2_valid[:, columns], in0=m2_valid[:, columns], scalar1=0.0)
+            nc.scalar.activation(out=result[:, columns], in_=m2_valid[:, columns], func=ACT.Sqrt, scale=inverse[:, 1:2])
+            nc.sync.dma_start(out=out[:, columns], in_=result[:, columns])
+
+        first_part, last_part = parts
+        mean_of(*first_part)
+        square_of(*first_part)
+        square_of(*last_part)
+        std_of(*first_part)
+        mean_of(*last_part)
+        std_of(*last_part)

@@ -32,9 +32,9 @@ PAD_WORD = -(1.0 + 0xBF80 / 2.0**23)
 FLOPS = 2 * SAMPLES * TOKENS * K * FEATURES
 
 VECTOR_TEST_GROUPS = 4
-VECTOR_COPY_GROUPS = 5
+VECTOR_COPY_GROUPS = 7
 WARM_UP_MATMULS = 4
-HOLD_MATMULS = 2
+HOLD_MATMULS = 1
 
 LEAD_TEST = 12
 LEAD_KEEP = 11
@@ -64,7 +64,7 @@ def tile_linearnnencoder_kernel(tc, x, W_words, W_scales, b, out):
             for half in (slice(0, 2 * K), slice(2 * K, 4 * K)):
                 nc.sync.dma_start(out=x_all[:, g, half], in_=group[:, half])
 
-        bias_rows_bf = const.tile([P, P], BF16)
+        bias_line = const.tile([P, FEATURES], BF16)
         ones_bf = const.tile([P, GROUP_ROWS], BF16)
         zero_col = const.tile([P, 1], F32)
         w_plane = const.tile([P, FEATURES], U8, align_bytes=64)
@@ -72,12 +72,12 @@ def tile_linearnnencoder_kernel(tc, x, W_words, W_scales, b, out):
         nc.vector.memset(zero_col[:], 0.0)
         nc.vector.memset(ones_bf[:], 1.0)
         nc.vector.memset(minus_pad_word[:], -PAD_WORD)
-        nc.vector.memset(bias_rows_bf[:], 0.0)
+        nc.vector.memset(bias_line[:], 0.0)
         nc.vector.memset(w_plane[:].bitcast(I32), 0)
 
         load_x(0)
-        nc.sync.dma_start(out=bias_rows_bf[0:F_TILES, :], in_=b.rearrange("(f c) -> f c", f=F_TILES))
         load_x(1)
+        nc.sync.dma_start(out=bias_line[0:1, :], in_=b.rearrange("(f c) -> f c", f=1))
         w_codes = const.tile([P, FEATURES * 4], U8, align_bytes=64)
         nc.sync.dma_start(
             out=w_codes[:].bitcast(I32),
@@ -90,8 +90,6 @@ def tile_linearnnencoder_kernel(tc, x, W_words, W_scales, b, out):
             )
         for g in range(2, GROUPS):
             load_x(g)
-        bias_everywhere = const.tile([P, FEATURES], BF16)
-        nc.sync.dma_start(out=bias_everywhere[:], in_=b.partition_broadcast(P))
 
         warm_col = const.tile([P, 1], F32)
         nc.scalar.activation(out=warm_col[:], in_=zero_col[:], func=ACT.Gelu)
@@ -111,13 +109,20 @@ def tile_linearnnencoder_kernel(tc, x, W_words, W_scales, b, out):
 
         unread_matmuls(WARM_UP_MATMULS)
 
-        bias_rows = const.tile([P, P], F32)
         bias = const.tile([P, F_TILES], F32)
         sample_of = const.tile([P, GROUP_SAMPLES], F32)
 
+        def bias_everywhere():
+            everywhere = psum_z.tile([P, FEATURES], F32, tag="z")
+            nc.tensor.matmul(out=everywhere[:], lhsT=ones_bf[:, 0:P], rhs=bias_line[:], start=True, stop=True)
+            return everywhere
+
         def spread_bias():
-            bias_ps = psum_z.tile([P, P], F32, tag="z")
-            nc.tensor.transpose(bias_ps[:], bias_rows[:], ident[:])
+            bias_ps = psum_z.tile([P, F_TILES, 32], F32, tag="z")
+            for f in range(F_TILES):
+                nc.tensor.matmul(
+                    out=bias_ps[:, f, :], lhsT=bias_line[:, f * P : (f + 1) * P], rhs=ones_bf[:, 0:32], start=True, stop=True
+                )
             return bias_ps
 
         stats = const.tile([P, F_TILES, SAMPLES, 3], F32)
@@ -269,9 +274,14 @@ def tile_linearnnencoder_kernel(tc, x, W_words, W_scales, b, out):
             nc.gpsimd.tensor_scalar_mul(out=all_over_n[:], in0=inverse[:, 0:1], scalar1=float(TOKENS))
             nc.gpsimd.tensor_sub(out=pads_over_n[:], in0=all_over_n[:], in1=positive[:, 0:1])
             nc.gpsimd.tensor_scalar_mul(out=minus_shift_weight[:], in0=pads_over_n[:], scalar1=-float(TOKENS))
+            nc.gpsimd.tensor_scalar(
+                out=pad_y_if_any[:], in0=pad_y[:], scalar1=positive[:, 0:1], scalar2=1.0, op0=ALU.mult, op1=ALU.mult
+            )
 
-        def gelu_of_padding():
-            nc.scalar.activation(out=pad_y[:], in_=bias_everywhere[:], func=ACT.Gelu)
+        def gelu_of_padding(everywhere):
+            nc.scalar.activation(out=pad_y[:], in_=everywhere[:], func=ACT.Gelu)
+
+        def gelu_of_padding_on_partitions():
             pad_y_column = const.tile([P, F_TILES], F32)
             nc.scalar.activation(out=pad_y_column[:], in_=bias[:], func=ACT.Gelu)
             nc.gpsimd.tensor_scalar(
@@ -306,8 +316,6 @@ def tile_linearnnencoder_kernel(tc, x, W_words, W_scales, b, out):
                         test_row(g, r)
                     if g == 0:
                         keep_valid_rows(g, keep[g], half)
-                if g == 0:
-                    nc.vector.tensor_copy(out=bias_rows[:], in_=bias_rows_bf[:])
                 if g == GROUPS - 1:
                     spread_counts()
             g = due(n, LEAD_KEEP)
@@ -317,35 +325,32 @@ def tile_linearnnencoder_kernel(tc, x, W_words, W_scales, b, out):
             if g is not None:
                 banks[g] = transpose_rows(g, keep[g])
                 if g == 0:
+                    everywhere = bias_everywhere()
                     unread_matmuls(HOLD_MATMULS)
                     bias_ps = spread_bias()
                 if g == GROUPS - 1:
-                    n_ps = count_valid_rows()
+                    weights_of_samples(count_valid_rows())
             g = due(n, LEAD_COPY)
             if g is not None:
                 grouped[g] = regroup(g, *banks[g])
+                if g == 0:
+                    gelu_of_padding(everywhere)
             g = due(n, LEAD_QUANTISE)
             if g is not None:
                 quantised[g] = quantise(grouped[g])
                 if g == 0:
-                    nc.vector.tensor_copy(out=bias[:], in_=bias_ps[:, 0:F_TILES])
-                if g == GROUPS - 1:
-                    weights_of_samples(n_ps)
-                    gelu_of_padding()
-                    nc.gpsimd.tensor_scalar(
-                        out=pad_y_if_any[:], in0=pad_y[:], scalar1=positive[:, 0:1], scalar2=1.0, op0=ALU.mult, op1=ALU.mult
-                    )
-
-        nc.scalar.activation(out=warm_col[:], in_=y[:, 0:1], func=ACT.Sqrt, scale=0.0)
+                    nc.vector.tensor_copy(out=bias[:], in_=bias_ps[:, :, 0])
+                if g == 1:
+                    gelu_of_padding_on_partitions()
 
         gap_squared = const.tile([P, FEATURES], F32)
         m2_valid = const.tile([P, FEATURES], F32)
         result = const.tile([P, 2 * FEATURES], F32)
-        parts = []
-        for first, last in ((0, F_TILES - 1), (F_TILES - 1, F_TILES)):
-            gap = psum_x.tile([P, F_TILES, P], F32, tag="xt_v")
-            m2_all = psum_x.tile([P, F_TILES, P], F32, tag="xt_s")
-            for f in range(first, last):
+
+        def turn(first, stop, pool, gap_tag, m2_tag):
+            gap = pool.tile([P, F_TILES, P], F32, tag=gap_tag)
+            m2_all = pool.tile([P, F_TILES, P], F32, tag=m2_tag)
+            for f in range(first, stop):
                 nc.tensor.matmul(
                     out=gap[:, f, :],
                     lhsT=minus_pad_y_column[:, f : f + 1].to_broadcast([P, P]),
@@ -354,25 +359,23 @@ def tile_linearnnencoder_kernel(tc, x, W_words, W_scales, b, out):
                     start=f == first,
                     stop=False,
                 )
-            for f in range(first, last):
+            for f in range(first, stop):
                 nc.tensor.matmul(
                     out=gap[:, f, :],
                     lhsT=stats[:, f, :, 1],
                     rhs=ident[:],
                     is_transpose=True,
                     start=False,
-                    stop=f == last - 1,
+                    stop=f == stop - 1,
                 )
-            for f in range(first, last):
+            for f in range(first, stop):
                 nc.tensor.transpose(m2_all[:, f, :], stats[:, f, :, 2], ident[:])
-            columns = slice(first * P, last * P)
-            parts.append(
-                (
-                    columns,
-                    slice(FEATURES + columns.start, FEATURES + columns.stop),
-                    gap[:].rearrange("s f o -> s (f o)")[:, columns],
-                    m2_all[:].rearrange("s f o -> s (f o)")[:, columns],
-                )
+            columns = slice(first * P, stop * P)
+            return (
+                columns,
+                slice(FEATURES + columns.start, FEATURES + columns.stop),
+                gap[:].rearrange("s f o -> s (f o)")[:, columns],
+                m2_all[:].rearrange("s f o -> s (f o)")[:, columns],
             )
 
         def mean_of(columns, mean_columns, gap_part, m2_part):
@@ -389,7 +392,7 @@ def tile_linearnnencoder_kernel(tc, x, W_words, W_scales, b, out):
         def square_of(columns, mean_columns, gap_part, m2_part):
             nc.scalar.activation(out=gap_squared[:, columns], in_=gap_part, func=ACT.Square)
 
-        def std_of(columns, mean_columns, gap_part, m2_part):
+        def deviation_of(columns, mean_columns, gap_part, m2_part):
             nc.vector.scalar_tensor_tensor(
                 out=m2_valid[:, columns],
                 in0=gap_squared[:, columns],
@@ -399,13 +402,21 @@ def tile_linearnnencoder_kernel(tc, x, W_words, W_scales, b, out):
                 op1=ALU.add,
             )
             nc.vector.tensor_scalar_max(out=m2_valid[:, columns], in0=m2_valid[:, columns], scalar1=0.0)
+
+        def root_of(columns, mean_columns, gap_part, m2_part):
             nc.scalar.activation(out=result[:, columns], in_=m2_valid[:, columns], func=ACT.Sqrt, scale=inverse[:, 1:2])
             nc.sync.dma_start(out=out[:, columns], in_=result[:, columns])
 
-        first_part, last_part = parts
-        mean_of(*first_part)
-        square_of(*first_part)
-        square_of(*last_part)
-        std_of(*first_part)
-        mean_of(*last_part)
-        std_of(*last_part)
+        nc.scalar.activation(out=warm_col[:], in_=y[:, 0:1], func=ACT.Sqrt, scale=0.0)
+        parts = (
+            turn(0, 2, psum_x, "xt_v", "xt_s"),
+            turn(2, 3, psum_x, "xt_v", "xt_s"),
+            turn(3, 4, psum_z, "z", "z"),
+        )
+        for part in parts:
+            mean_of(*part)
+        for part in parts:
+            square_of(*part)
+        for part in parts:
+            deviation_of(*part)
+            root_of(*part)

@@ -31,16 +31,16 @@ PAD_WORD = -(1.0 + 0xBF80 / 2.0**23)
 
 FLOPS = 2 * SAMPLES * TOKENS * K * FEATURES
 
-VECTOR_TEST_GROUPS = 4
-VECTOR_COPY_GROUPS = 7
+VECTOR_TEST_GROUPS = 3
+VECTOR_COPY_GROUPS = 5
 WARM_UP_MATMULS = 4
-HOLD_MATMULS = 1
+HOLD_MATMULS = 2
 
-LEAD_TEST = 12
-LEAD_KEEP = 11
-LEAD_TRANSPOSE = 7
-LEAD_COPY = 6
-LEAD_QUANTISE = 5
+LEAD_TEST = 11
+LEAD_KEEP = 10
+LEAD_TRANSPOSE = 6
+LEAD_COPY = 5
+LEAD_QUANTISE = 4
 
 
 def tile_linearnnencoder_kernel(tc, x, W_words, W_scales, b, out):
@@ -78,6 +78,7 @@ def tile_linearnnencoder_kernel(tc, x, W_words, W_scales, b, out):
         load_x(0)
         load_x(1)
         nc.sync.dma_start(out=bias_line[0:1, :], in_=b.rearrange("(f c) -> f c", f=1))
+        load_x(2)
         w_codes = const.tile([P, FEATURES * 4], U8, align_bytes=64)
         nc.sync.dma_start(
             out=w_codes[:].bitcast(I32),
@@ -88,7 +89,7 @@ def tile_linearnnencoder_kernel(tc, x, W_words, W_scales, b, out):
                 out=w_plane[32 * quadrant : 32 * quadrant + 4, :].bitcast(I32),
                 in_=W_scales[0, 4 * quadrant : 4 * quadrant + 4, :].bitcast(I32),
             )
-        for g in range(2, GROUPS):
+        for g in range(3, GROUPS):
             load_x(g)
 
         warm_col = const.tile([P, 1], F32)
@@ -274,12 +275,12 @@ def tile_linearnnencoder_kernel(tc, x, W_words, W_scales, b, out):
             nc.gpsimd.tensor_scalar_mul(out=all_over_n[:], in0=inverse[:, 0:1], scalar1=float(TOKENS))
             nc.gpsimd.tensor_sub(out=pads_over_n[:], in0=all_over_n[:], in1=positive[:, 0:1])
             nc.gpsimd.tensor_scalar_mul(out=minus_shift_weight[:], in0=pads_over_n[:], scalar1=-float(TOKENS))
-            nc.gpsimd.tensor_scalar(
-                out=pad_y_if_any[:], in0=pad_y[:], scalar1=positive[:, 0:1], scalar2=1.0, op0=ALU.mult, op1=ALU.mult
-            )
 
         def gelu_of_padding(everywhere):
             nc.scalar.activation(out=pad_y[:], in_=everywhere[:], func=ACT.Gelu)
+            nc.gpsimd.tensor_scalar(
+                out=pad_y_if_any[:], in0=pad_y[:], scalar1=positive[:, 0:1], scalar2=1.0, op0=ALU.mult, op1=ALU.mult
+            )
 
         def gelu_of_padding_on_partitions():
             pad_y_column = const.tile([P, F_TILES], F32)
@@ -325,7 +326,6 @@ def tile_linearnnencoder_kernel(tc, x, W_words, W_scales, b, out):
             if g is not None:
                 banks[g] = transpose_rows(g, keep[g])
                 if g == 0:
-                    everywhere = bias_everywhere()
                     unread_matmuls(HOLD_MATMULS)
                     bias_ps = spread_bias()
                 if g == GROUPS - 1:
@@ -333,8 +333,6 @@ def tile_linearnnencoder_kernel(tc, x, W_words, W_scales, b, out):
             g = due(n, LEAD_COPY)
             if g is not None:
                 grouped[g] = regroup(g, *banks[g])
-                if g == 0:
-                    gelu_of_padding(everywhere)
             g = due(n, LEAD_QUANTISE)
             if g is not None:
                 quantised[g] = quantise(grouped[g])
@@ -342,6 +340,9 @@ def tile_linearnnencoder_kernel(tc, x, W_words, W_scales, b, out):
                     nc.vector.tensor_copy(out=bias[:], in_=bias_ps[:, :, 0])
                 if g == 1:
                     gelu_of_padding_on_partitions()
+
+            if n == F_TILES * (GROUPS - 2):
+                gelu_of_padding(bias_everywhere())
 
         gap_squared = const.tile([P, FEATURES], F32)
         m2_valid = const.tile([P, FEATURES], F32)
@@ -401,6 +402,8 @@ def tile_linearnnencoder_kernel(tc, x, W_words, W_scales, b, out):
                 op0=ALU.mult,
                 op1=ALU.add,
             )
+
+        def at_least_zero(columns, mean_columns, gap_part, m2_part):
             nc.vector.tensor_scalar_max(out=m2_valid[:, columns], in0=m2_valid[:, columns], scalar1=0.0)
 
         def root_of(columns, mean_columns, gap_part, m2_part):
@@ -413,10 +416,18 @@ def tile_linearnnencoder_kernel(tc, x, W_words, W_scales, b, out):
             turn(2, 3, psum_x, "xt_v", "xt_s"),
             turn(3, 4, psum_z, "z", "z"),
         )
-        for part in parts:
-            mean_of(*part)
+        first, second, third = parts
+        mean_of(*first)
+        mean_of(*second)
         for part in parts:
             square_of(*part)
-        for part in parts:
-            deviation_of(*part)
-            root_of(*part)
+        deviation_of(*first)
+        deviation_of(*second)
+        at_least_zero(*first)
+        root_of(*first)
+        deviation_of(*third)
+        at_least_zero(*second)
+        root_of(*second)
+        at_least_zero(*third)
+        root_of(*third)
+        mean_of(*third)

@@ -321,23 +321,26 @@ def tile_linearnnencoder_kernel(tc, x, W_words, W_scales, b, out):
                     spread_counts()
             g = due(n, LEAD_KEEP)
             if g is not None and g > 0:
-                keep_valid_rows(g, keep[g], range(ROWS_PER_PARTITION))
+                keep_valid_rows(g, keep[g], (0, 1) if g == 1 else range(ROWS_PER_PARTITION))
             g = due(n, LEAD_TRANSPOSE)
             if g is not None:
                 banks[g] = transpose_rows(g, keep[g])
                 if g == 0:
                     unread_matmuls(HOLD_MATMULS)
                     bias_ps = spread_bias()
+                if g == 1:
+                    unread_matmuls(1)
                 if g == GROUPS - 1:
                     weights_of_samples(count_valid_rows())
             g = due(n, LEAD_COPY)
             if g is not None:
                 grouped[g] = regroup(g, *banks[g])
+                if g == 0:
+                    keep_valid_rows(1, keep[1], (2, 3))
+                    nc.vector.tensor_copy(out=bias[:], in_=bias_ps[:, :, 0])
             g = due(n, LEAD_QUANTISE)
             if g is not None:
                 quantised[g] = quantise(grouped[g])
-                if g == 0:
-                    nc.vector.tensor_copy(out=bias[:], in_=bias_ps[:, :, 0])
                 if g == 1:
                     gelu_of_padding_on_partitions()
 
@@ -417,8 +420,6 @@ def tile_linearnnencoder_kernel(tc, x, W_words, W_scales, b, out):
             turn(3, 4, psum_z, "z", "z"),
         )
         first, second, third = parts
-        mean_of(*first)
-        mean_of(*second)
         for part in parts:
             square_of(*part)
         deviation_of(*first)
@@ -430,4 +431,5 @@ def tile_linearnnencoder_kernel(tc, x, W_words, W_scales, b, out):
         root_of(*second)
         at_least_zero(*third)
         root_of(*third)
-        mean_of(*third)
+        for part in parts:
+            mean_of(*part)

@@ -32,15 +32,16 @@ PAD_WORD = -(1.0 + 0xBF80 / 2.0**23)
 FLOPS = 2 * SAMPLES * TOKENS * K * FEATURES
 
 VECTOR_TEST_GROUPS = 3
-VECTOR_COPY_GROUPS = 5
+VECTOR_COPY_GROUPS = 6
 WARM_UP_MATMULS = 4
 HOLD_MATMULS = 2
 
 LEAD_TEST = 11
-LEAD_KEEP = 10
-LEAD_TRANSPOSE = 6
-LEAD_COPY = 5
-LEAD_QUANTISE = 4
+LEAD_KEEP = 11
+LEAD_TRANSPOSE = 7
+LEAD_VECTOR_COPY = 7
+LEAD_SCALAR_COPY = 6
+LEAD_QUANTISE = 6
 
 
 def tile_linearnnencoder_kernel(tc, x, W_words, W_scales, b, out):
@@ -134,7 +135,7 @@ def tile_linearnnencoder_kernel(tc, x, W_words, W_scales, b, out):
 
         def test_row(g, r):
             words = x_words(g)[:, r * WORDS : (r + 1) * WORDS]
-            if g < VECTOR_TEST_GROUPS and r % 2 == 1:
+            if g < VECTOR_TEST_GROUPS and r == ROWS_PER_PARTITION - 1:
                 unlike = acts.tile([P, WORDS], BF16)
                 nc.vector.tensor_scalar(
                     out=unlike[:],
@@ -179,15 +180,9 @@ def tile_linearnnencoder_kernel(tc, x, W_words, W_scales, b, out):
                     )
             return xt_v, xt_s
 
-        def regroup(g, xt_v, xt_s):
-            grouped = stage.tile([P, ROWS_PER_PARTITION, P, 4], BF16, align_bytes=64)
+        def regroup(grouped, half, bank, copy):
             grouped_words = grouped[:].bitcast(F32)
-            if g < VECTOR_COPY_GROUPS:
-                nc.vector.tensor_copy(out=grouped_words[:, 0:2, :, :], in_=xt_v[:].rearrange("j r u p -> j r p u"))
-            else:
-                nc.scalar.copy(out=grouped_words[:, 0:2, :, :], in_=xt_v[:].rearrange("j r u p -> j r p u"))
-            nc.scalar.copy(out=grouped_words[:, 2:4, :, :], in_=xt_s[:].rearrange("j r u p -> j r p u"))
-            return grouped
+            copy(out=grouped_words[:, 2 * half : 2 * half + 2, :, :], in_=bank[:].rearrange("j r u p -> j r p u"))
 
         def quantise(grouped):
             x_codes = stage.tile([P, GROUP_ROWS], U32, align_bytes=64)
@@ -321,7 +316,7 @@ def tile_linearnnencoder_kernel(tc, x, W_words, W_scales, b, out):
                     spread_counts()
             g = due(n, LEAD_KEEP)
             if g is not None and g > 0:
-                keep_valid_rows(g, keep[g], (0, 1) if g == 1 else range(ROWS_PER_PARTITION))
+                keep_valid_rows(g, keep[g], range(ROWS_PER_PARTITION))
             g = due(n, LEAD_TRANSPOSE)
             if g is not None:
                 banks[g] = transpose_rows(g, keep[g])
@@ -332,15 +327,21 @@ def tile_linearnnencoder_kernel(tc, x, W_words, W_scales, b, out):
                     unread_matmuls(1)
                 if g == GROUPS - 1:
                     weights_of_samples(count_valid_rows())
-            g = due(n, LEAD_COPY)
+            g = due(n, LEAD_VECTOR_COPY)
             if g is not None:
-                grouped[g] = regroup(g, *banks[g])
-                if g == 0:
-                    keep_valid_rows(1, keep[1], (2, 3))
-                    nc.vector.tensor_copy(out=bias[:], in_=bias_ps[:, :, 0])
+                grouped[g] = stage.tile([P, ROWS_PER_PARTITION, P, 4], BF16, name="grouped", align_bytes=64)
+                if g < VECTOR_COPY_GROUPS:
+                    regroup(grouped[g], 0, banks[g][0], nc.vector.tensor_copy)
+                else:
+                    regroup(grouped[g], 0, banks[g][0], nc.scalar.copy)
+            g = due(n, LEAD_SCALAR_COPY)
+            if g is not None:
+                regroup(grouped[g], 1, banks[g][1], nc.scalar.copy)
             g = due(n, LEAD_QUANTISE)
             if g is not None:
                 quantised[g] = quantise(grouped[g])
+                if g == 0:
+                    nc.vector.tensor_copy(out=bias[:], in_=bias_ps[:, :, 0])
                 if g == 1:
                     gelu_of_padding_on_partitions()
 

@@ -29,11 +29,13 @@ PARTITIONS_PER_SAMPLE = TOKENS // ROWS_PER_PARTITION
 
 PAD_WORD = -(1.0 + 0xBF80 / 2.0**23)
 
+ONES_WORD = 0x3F803F80
+
 FLOPS = 2 * SAMPLES * TOKENS * K * FEATURES
 
 VECTOR_TEST_GROUPS = 3
 VECTOR_COPY_GROUPS = 6
-WARM_UP_MATMULS = 4
+WARM_UP_MATMULS = 7
 HOLD_MATMULS = 2
 
 LEAD_TEST = 11
@@ -66,13 +68,15 @@ def tile_linearnnencoder_kernel(tc, x, W_words, W_scales, b, out):
                 nc.sync.dma_start(out=x_all[:, g, half], in_=group[:, half])
 
         bias_line = const.tile([P, FEATURES], BF16)
-        ones_bf = const.tile([P, GROUP_ROWS], BF16)
+        ones_bf = const.tile([P, P], BF16)
+        warm_bf = const.tile([P, GROUP_ROWS], BF16)
         zero_col = const.tile([P, 1], F32)
         w_plane = const.tile([P, FEATURES], U8, align_bytes=64)
         minus_pad_word = const.tile([P, 1], F32)
         nc.vector.memset(zero_col[:], 0.0)
-        nc.vector.memset(ones_bf[:], 1.0)
+        nc.vector.memset(warm_bf[:].bitcast(I32), ONES_WORD)
         nc.vector.memset(minus_pad_word[:], -PAD_WORD)
+        nc.vector.memset(ones_bf[:], 1.0)
         nc.vector.memset(bias_line[:], 0.0)
         nc.vector.memset(w_plane[:].bitcast(I32), 0)
 
@@ -107,7 +111,7 @@ def tile_linearnnencoder_kernel(tc, x, W_words, W_scales, b, out):
         def unread_matmuls(count):
             unread = psum_z.tile([P, GROUP_ROWS], F32, tag="z")
             for repeat in range(count):
-                nc.tensor.matmul(out=unread[:], lhsT=ones_bf[:, 0:P], rhs=ones_bf[:], start=True, stop=True)
+                nc.tensor.matmul(out=unread[:], lhsT=warm_bf[:, 0:P], rhs=warm_bf[:], start=True, stop=True)
 
         unread_matmuls(WARM_UP_MATMULS)
 
@@ -116,7 +120,7 @@ def tile_linearnnencoder_kernel(tc, x, W_words, W_scales, b, out):
 
         def bias_everywhere():
             everywhere = psum_z.tile([P, FEATURES], F32, tag="z")
-            nc.tensor.matmul(out=everywhere[:], lhsT=ones_bf[:, 0:P], rhs=bias_line[:], start=True, stop=True)
+            nc.tensor.matmul(out=everywhere[:], lhsT=ones_bf[:], rhs=bias_line[:], start=True, stop=True)
             return everywhere
 
         def spread_bias():
@@ -323,8 +327,6 @@ def tile_linearnnencoder_kernel(tc, x, W_words, W_scales, b, out):
                 if g == 0:
                     unread_matmuls(HOLD_MATMULS)
                     bias_ps = spread_bias()
-                if g == 1:
-                    unread_matmuls(1)
                 if g == GROUPS - 1:
                     weights_of_samples(count_valid_rows())
             g = due(n, LEAD_VECTOR_COPY)

@@ -33,7 +33,7 @@ ONES_WORD = 0x3F803F80
 
 FLOPS = 2 * SAMPLES * TOKENS * K * FEATURES
 
-VECTOR_TEST_GROUPS = 3
+VECTOR_TEST_GROUPS = 4
 VECTOR_COPY_GROUPS = 6
 WARM_UP_MATMULS = 7
 HOLD_MATMULS = 2
@@ -64,8 +64,9 @@ def tile_linearnnencoder_kernel(tc, x, W_words, W_scales, b, out):
             group = rows[g * GROUP_ROWS : (g + 1) * GROUP_ROWS, :].rearrange(
                 "(p r) k -> p (r k)", r=ROWS_PER_PARTITION
             )
-            for half in (slice(0, 2 * K), slice(2 * K, 4 * K)):
-                nc.sync.dma_start(out=x_all[:, g, half], in_=group[:, half])
+            piece = K if g == 0 else 2 * K
+            for start in range(0, ROWS_PER_PARTITION * K, piece):
+                nc.sync.dma_start(out=x_all[:, g, start : start + piece], in_=group[:, start : start + piece])
 
         bias_line = const.tile([P, FEATURES], BF16)
         ones_bf = const.tile([P, P], BF16)

@@ -201,7 +201,7 @@ def tile_linearnnencoder_kernel(tc, x, W_words, W_scales, b, out):
 
         def multiply(g, f, x_codes, x_plane):
             z = psum_z.tile([P, GROUP_ROWS], F32)
-            for repeat in range(1 if g == 0 and f == 0 else 2):
+            for repeat in range(1 if f >= F_TILES // 2 or (g == 0 and f == 0) else 2):
                 nc.tensor.matmul_mx(
                     out=z[:],
                     lhsT=w_codes[:, f * P * 4 : (f + 1) * P * 4].bitcast(FP8X4),

from contextlib import ExitStack

import concourse.mybir as mybir
from concourse.masks import make_identity

F32 = mybir.dt.float32
BF16 = mybir.dt.bfloat16
I32 = mybir.dt.int32
U32 = mybir.dt.uint32
U8 = mybir.dt.uint8
FP8X4 = mybir.dt.float8_e4m3fn_x4
ACT = mybir.ActivationFunctionType
ALU = mybir.AluOpType
AX = mybir.AxisListType

P = 128
SAMPLES = 128
TOKENS = 32
K = 512
FEATURES = 512
F_TILES = FEATURES // P
WORDS = K // 2

GROUP_ROWS = 512
GROUPS = SAMPLES * TOKENS // GROUP_ROWS
GROUP_SAMPLES = GROUP_ROWS // TOKENS
ROWS_PER_PARTITION = GROUP_ROWS // P
PARTITIONS_PER_SAMPLE = TOKENS // ROWS_PER_PARTITION

PAD_WORD = -(1.0 + 0xBF80 / 2.0**23)

ONES_WORD = 0x3F803F80

FLOPS = 2 * SAMPLES * TOKENS * K * FEATURES

VECTOR_TEST_GROUPS = 4
VECTOR_COPY_GROUPS = 6
WARM_UP_MATMULS = 7
HOLD_MATMULS = 2

LEAD_TEST = 11
LEAD_KEEP = 11
LEAD_TRANSPOSE = 7
LEAD_VECTOR_COPY = 7
LEAD_SCALAR_COPY = 6
LEAD_QUANTISE = 6


def tile_linearnnencoder_kernel(tc, x, W_words, W_scales, b, out):
    nc = tc.nc
    rows = x.flatten_outer_dims()

    with ExitStack() as scopes:
        const = scopes.enter_context(tc.tile_pool(name="const", bufs=1))
        stage = scopes.enter_context(tc.tile_pool(name="stage", bufs=3))
        acts = scopes.enter_context(tc.tile_pool(name="acts", bufs=8))
        psum_x = scopes.enter_context(tc.psum_pool(name="psum_x", bufs=2))
        psum_z = scopes.enter_context(tc.psum_pool(name="psum_z", bufs=4))
        scopes.enter_context(tc.manual_schedule())

        x_all = const.tile([P, GROUPS, ROWS_PER_PARTITION * K], BF16)

        def load_x(g):
            group = rows[g * GROUP_ROWS : (g + 1) * GROUP_ROWS, :].rearrange(
                "(p r) k -> p (r k)", r=ROWS_PER_PARTITION
            )
            piece = K if g == 0 else 2 * K
            for start in range(0, ROWS_PER_PARTITION * K, piece):
                nc.sync.dma_start(out=x_all[:, g, start : start + piece], in_=group[:, start : start + piece])

        bias_line = const.tile([P, FEATURES], BF16)
        ones_bf = const.tile([P, P], BF16)
        warm_bf = const.tile([P, GROUP_ROWS], BF16)
        zero_col = const.tile([P, 1], F32)
        w_plane = const.tile([P, FEATURES], U8, align_bytes=64)
        minus_pad_word = const.tile([P, 1], F32)
        nc.vector.memset(zero_col[:], 0.0)
        nc.vector.memset(warm_bf[:].bitcast(I32), ONES_WORD)
        nc.vector.memset(minus_pad_word[:], -PAD_WORD)
        nc.vector.memset(ones_bf[:], 1.0)
        nc.vector.memset(bias_line[:], 0.0)
        nc.vector.memset(w_plane[:].bitcast(I32), 0)

        load_x(0)
        load_x(1)
        nc.sync.dma_start(out=bias_line[0:1, :], in_=b.rearrange("(f c) -> f c", f=1))
        load_x(2)
        w_codes = const.tile([P, FEATURES * 4], U8, align_bytes=64)
        nc.sync.dma_start(
            out=w_codes[:].bitcast(I32),
            in_=W_words.rearrange("o p n t -> p (o n t)").bitcast(I32),
        )
        for quadrant in range(4):
            nc.sync.dma_start(
                out=w_plane[32 * quadrant : 32 * quadrant + 4, :].bitcast(I32),
                in_=W_scales[0, 4 * quadrant : 4 * quadrant + 4, :].bitcast(I32),
            )
        for g in range(3, GROUPS):
            load_x(g)

        warm_col = const.tile([P, 1], F32)
        nc.scalar.activation(out=warm_col[:], in_=zero_col[:], func=ACT.Gelu)

        ident = const.tile([P, P], F32)
        make_identity(nc, ident[:])
        minus_ones = const.tile([P, 2], F32)
        nc.gpsimd.memset(minus_ones[:], -1.0)
        zero_and_one = const.tile([P, 2], F32)
        nc.gpsimd.memset(zero_and_one[:, 0:1], 0.0)
        nc.gpsimd.memset(zero_and_one[:, 1:2], 1.0)

        def unread_matmuls(count):
            unread = psum_z.tile([P, GROUP_ROWS], F32, tag="z")
            for repeat in range(count):
                nc.tensor.matmul(out=unread[:], lhsT=warm_bf[:, 0:P], rhs=warm_bf[:], start=True, stop=True)

        unread_matmuls(WARM_UP_MATMULS)

        bias = const.tile([P, F_TILES], F32)
        sample_of = const.tile([P, GROUP_SAMPLES], F32)

        def bias_everywhere():
            everywhere = psum_z.tile([P, FEATURES], F32, tag="z")
            nc.tensor.matmul(out=everywhere[:], lhsT=ones_bf[:], rhs=bias_line[:], start=True, stop=True)
            return everywhere

        def spread_bias():
            bias_ps = psum_z.tile([P, F_TILES, 32], F32, tag="z")
            for f in range(F_TILES):
                nc.tensor.matmul(
                    out=bias_ps[:, f, :], lhsT=bias_line[:, f * P : (f + 1) * P], rhs=ones_bf[:, 0:32], start=True, stop=True
                )
            return bias_ps

        stats = const.tile([P, F_TILES, SAMPLES, 3], F32)
        distance = const.tile([P, GROUPS, ROWS_PER_PARTITION], F32)

        def x_words(g):
            return x_all[:, g, :].bitcast(F32)

        def test_row(g, r):
            words = x_words(g)[:, r * WORDS : (r + 1) * WORDS]
            if g < VECTOR_TEST_GROUPS and r == ROWS_PER_PARTITION - 1:
                unlike = acts.tile([P, WORDS], BF16)
                nc.vector.tensor_scalar(
                    out=unlike[:],
                    in0=words,
                    scalar1=PAD_WORD,
                    scalar2=0.0,
                    op0=ALU.not_equal,
                    op1=ALU.add,
                    accum_out=distance[:, g, r : r + 1],
                )
            else:
                squares = acts.tile([P, WORDS], BF16)
                nc.scalar.activation(
                    out=squares[:],
                    in_=words,
                    func=ACT.Square,
                    bias=minus_pad_word[:],
                    accum_out=distance[:, g, r : r + 1],
                )

        def keep_valid_rows(g, keep_rows, of_rows):
            for r in of_rows:
                nc.vector.tensor_scalar(
                    out=keep_rows[:, r, :],
                    in0=ident[:],
                    scalar1=distance[:, g, r : r + 1],
                    scalar2=0.0,
                    op0=ALU.mult,
                    op1=ALU.is_gt,
                )

        def transpose_rows(g, keep_rows):
            xt_v = psum_x.tile([P, 2, 2, P], F32)
            xt_s = psum_x.tile([P, 2, 2, P], F32)
            for r in range(ROWS_PER_PARTITION):
                xt = xt_v if r < 2 else xt_s
                for u in range(2):
                    nc.tensor.transpose(
                        xt[:, r % 2, u, :],
                        x_words(g)[:, r * WORDS + u : (r + 1) * WORDS : 2],
                        keep_rows[:, r, :],
                    )
            return xt_v, xt_s

        def regroup(grouped, half, bank, copy):
            grouped_words = grouped[:].bitcast(F32)
            copy(out=grouped_words[:, 2 * half : 2 * half + 2, :, :], in_=bank[:].rearrange("j r u p -> j r p u"))

        def quantise(grouped):
            x_codes = stage.tile([P, GROUP_ROWS], U32, align_bytes=64)
            x_plane = stage.tile([P, GROUP_ROWS], U8, align_bytes=64)
            nc.vector.quantize_mx(
                out=x_codes[:].bitcast(FP8X4),
                scales=x_plane[:],
                in_=grouped[:].rearrange("j r p t -> j (r p t)"),
            )
            return x_codes, x_plane

        def multiply(g, f, x_codes, x_plane):
            z = psum_z.tile([P, GROUP_ROWS], F32)
            for repeat in range(1 if f >= F_TILES // 2 or (g == 0 and f == 0) else 2):
                nc.tensor.matmul_mx(
                    out=z[:],
                    lhsT=w_codes[:, f * P * 4 : (f + 1) * P * 4].bitcast(FP8X4),
                    lhsT_scale=w_plane[:, f * P : (f + 1) * P],
                    rhs=x_codes[:].bitcast(FP8X4),
                    rhs_scale=x_plane[:],
                    start=True,
                    stop=True,
                )
            return z

        def gelu(f, z):
            y = acts.tile([P, GROUP_ROWS], F32)
            nc.scalar.activation(out=y[:], in_=z[:], func=ACT.Gelu, bias=bias[:, f : f + 1])
            return y

        def statistics(g, f, y):
            y_by_sample = y[:].rearrange("o (r s h) -> o r s h", r=ROWS_PER_PARTITION, s=GROUP_SAMPLES)
            for pair in range(GROUP_SAMPLES // 2):
                s = g * GROUP_SAMPLES + 2 * pair
                nc.vector.bn_stats(
                    out=stats[:, f, s : s + 2, :].rearrange("o e kind -> o (e kind)"),
                    in_=y_by_sample[:, :, 2 * pair : 2 * pair + 2, :].rearrange("o r e h -> o r h e"),
                )

        def column(name):
            return const.tile([P, 1], F32, name=name)

        all_over_n = column("all_over_n")
        pads_over_n = column("pads_over_n")
        minus_shift_weight = column("minus_shift_weight")
        positive = const.tile([P, 2], F32)
        inverse = const.tile([P, 2], F32)
        pad_y = const.tile([P, FEATURES], F32)
        pad_y_if_any = const.tile([P, FEATURES], F32)
        minus_pad_y_column = const.tile([P, F_TILES], F32)
        spread = const.tile([P, GROUPS, GROUP_SAMPLES], BF16)

        def spread_counts():
            is_valid = const.tile([P, GROUPS, ROWS_PER_PARTITION], F32)
            nc.gpsimd.tensor_single_scalar(out=is_valid[:], in_=distance[:], scalar=0.0, op=ALU.is_gt)
            valid_of_2 = const.tile([P, GROUPS, 2], F32)
            nc.gpsimd.tensor_add(out=valid_of_2[:], in0=is_valid[:, :, 0:2], in1=is_valid[:, :, 2:4])
            valid_here = const.tile([P, GROUPS, 1], F32)
            nc.gpsimd.tensor_add(out=valid_here[:], in0=valid_of_2[:, :, 0:1], in1=valid_of_2[:, :, 1:2])
            nc.gpsimd.tensor_tensor(
                out=spread[:],
                in0=valid_here[:].to_broadcast([P, GROUPS, GROUP_SAMPLES]),
                in1=sample_of[:].unsqueeze(1).to_broadcast([P, GROUPS, GROUP_SAMPLES]),
                op=ALU.mult,
            )

        def count_valid_rows():
            n_ps = psum_z.tile([P, 32], F32, tag="z")
            nc.tensor.matmul(
                out=n_ps[:], lhsT=spread[:].rearrange("p g s -> p (g s)"), rhs=ones_bf[:, 0:32], start=True, stop=True
            )
            return n_ps

        def weights_of_samples(n_ps):
            n_twice = const.tile([P, 2], F32)
            nc.vector.tensor_copy(out=n_twice[:], in_=n_ps[:, 0:2])
            divisors = const.tile([P, 2], F32)
            nc.gpsimd.tensor_sub(out=divisors[:], in0=n_twice[:], in1=zero_and_one[:])
            nc.gpsimd.tensor_scalar(
                out=positive[:], in0=divisors[:], scalar1=1.0, scalar2=0.0, op0=ALU.min, op1=ALU.max
            )
            nc.gpsimd.tensor_scalar_max(out=divisors[:], in0=divisors[:], scalar1=1.0)
            nc.gpsimd.tensor_tensor(out=inverse[:], in0=divisors[:], in1=minus_ones[:], op=ALU.pow)
            nc.gpsimd.tensor_mul(out=inverse[:], in0=inverse[:], in1=positive[:])
            nc.gpsimd.tensor_scalar_mul(out=all_over_n[:], in0=inverse[:, 0:1], scalar1=float(TOKENS))
            nc.gpsimd.tensor_sub(out=pads_over_n[:], in0=all_over_n[:], in1=positive[:, 0:1])
            nc.gpsimd.tensor_scalar_mul(out=minus_shift_weight[:], in0=pads_over_n[:], scalar1=-float(TOKENS))

        def gelu_of_padding(everywhere):
            nc.scalar.activation(out=pad_y[:], in_=everywhere[:], func=ACT.Gelu)
            nc.gpsimd.tensor_scalar(
                out=pad_y_if_any[:], in0=pad_y[:], scalar1=positive[:, 0:1], scalar2=1.0, op0=ALU.mult, op1=ALU.mult
            )

        def gelu_of_padding_on_partitions():
            pad_y_column = const.tile([P, F_TILES], F32)
            nc.scalar.activation(out=pad_y_column[:], in_=bias[:], func=ACT.Gelu)
            nc.gpsimd.tensor_scalar(
                out=minus_pad_y_column[:], in0=pad_y_column[:], scalar1=-1.0, scalar2=1.0, op0=ALU.mult, op1=ALU.mult
            )

        keep = {}
        banks = {}
        grouped = {}
        quantised = {}
        nc.vector.tensor_reduce(
            out=sample_of[:],
            in_=ident[:].rearrange("p (s h) -> p s h", h=PARTITIONS_PER_SAMPLE),
            axis=AX.X,
            op=ALU.add,
        )

        def due(step, lead):
            g, rest = divmod(step + lead, F_TILES)
            return g if rest == 0 and 0 <= g < GROUPS else None

        for n in range(-LEAD_TEST, F_TILES * GROUPS):
            if n >= 0:
                g, f = divmod(n, F_TILES)
                y = gelu(f, multiply(g, f, *quantised[g]))
                statistics(g, f, y)
            g = due(n, LEAD_TEST)
            if g is not None:
                keep[g] = stage.tile([P, ROWS_PER_PARTITION, P], F32, name="keep_rows", bufs=2)
                for half in ((0, 1), (2, 3)):
                    for r in half:
                        test_row(g, r)
                    if g == 0:
                        keep_valid_rows(g, keep[g], half)
                if g == GROUPS - 1:
                    spread_counts()
            g = due(n, LEAD_KEEP)
            if g is not None and g > 0:
                keep_valid_rows(g, keep[g], range(ROWS_PER_PARTITION))
            g = due(n, LEAD_TRANSPOSE)
            if g is not None:
                banks[g] = transpose_rows(g, keep[g])
                if g == 0:
                    unread_matmuls(HOLD_MATMULS)
                    bias_ps = spread_bias()
                if g == GROUPS - 1:
                    weights_of_samples(count_valid_rows())
            g = due(n, LEAD_VECTOR_COPY)
            if g is not None:
                grouped[g] = stage.tile([P, ROWS_PER_PARTITION, P, 4], BF16, name="grouped", align_bytes=64)
                if g < VECTOR_COPY_GROUPS:
                    regroup(grouped[g], 0, banks[g][0], nc.vector.tensor_copy)
                else:
                    regroup(grouped[g], 0, banks[g][0], nc.scalar.copy)
            g = due(n, LEAD_SCALAR_COPY)
            if g is not None:
                regroup(grouped[g], 1, banks[g][1], nc.scalar.copy)
            g = due(n, LEAD_QUANTISE)
            if g is not None:
                quantised[g] = quantise(grouped[g])
                if g == 0:
                    nc.vector.tensor_copy(out=bias[:], in_=bias_ps[:, :, 0])
                if g == 1:
                    gelu_of_padding_on_partitions()

            if n == F_TILES * (GROUPS - 2):
                gelu_of_padding(bias_everywhere())

        gap_squared = const.tile([P, FEATURES], F32)
        m2_valid = const.tile([P, FEATURES], F32)
        result = const.tile([P, 2 * FEATURES], F32)

        def turn(first, stop, pool, gap_tag, m2_tag):
            gap = pool.tile([P, F_TILES, P], F32, tag=gap_tag)
            m2_all = pool.tile([P, F_TILES, P], F32, tag=m2_tag)
            for f in range(first, stop):
                nc.tensor.matmul(
                    out=gap[:, f, :],
                    lhsT=minus_pad_y_column[:, f : f + 1].to_broadcast([P, P]),
                    rhs=ident[:],
                    is_transpose=True,
                    start=f == first,
                    stop=False,
                )
            for f in range(first, stop):
                nc.tensor.matmul(
                    out=gap[:, f, :],
                    lhsT=stats[:, f, :, 1],
                    rhs=ident[:],
                    is_transpose=True,
                    start=False,
                    stop=f == stop - 1,
                )
            for f in range(first, stop):
                nc.tensor.transpose(m2_all[:, f, :], stats[:, f, :, 2], ident[:])
            columns = slice(first * P, stop * P)
            return (
                columns,
                slice(FEATURES + columns.start, FEATURES + columns.stop),
                gap[:].rearrange("s f o -> s (f o)")[:, columns],
                m2_all[:].rearrange("s f o -> s (f o)")[:, columns],
            )

        def mean_of(columns, mean_columns, gap_part, m2_part):
            nc.vector.scalar_tensor_tensor(
                out=result[:, mean_columns],
                in0=gap_part,
                scalar=all_over_n[:],
                in1=pad_y_if_any[:, columns],
                op0=ALU.mult,
                op1=ALU.add,
            )
            nc.sync.dma_start(out=out[:, mean_columns], in_=result[:, mean_columns])

        def square_of(columns, mean_columns, gap_part, m2_part):
            nc.scalar.activation(out=gap_squared[:, columns], in_=gap_part, func=ACT.Square)

        def deviation_of(columns, mean_columns, gap_part, m2_part):
            nc.vector.scalar_tensor_tensor(
                out=m2_valid[:, columns],
                in0=gap_squared[:, columns],
                scalar=minus_shift_weight[:],
                in1=m2_part,
                op0=ALU.mult,
                op1=ALU.add,
            )

        def at_least_zero(columns, mean_columns, gap_part, m2_part):
            nc.vector.tensor_scalar_max(out=m2_valid[:, columns], in0=m2_valid[:, columns], scalar1=0.0)

        def root_of(columns, mean_columns, gap_part, m2_part):
            nc.scalar.activation(out=result[:, columns], in_=m2_valid[:, columns], func=ACT.Sqrt, scale=inverse[:, 1:2])
            nc.sync.dma_start(out=out[:, columns], in_=result[:, columns])

        nc.scalar.activation(out=warm_col[:], in_=y[:, 0:1], func=ACT.Sqrt, scale=0.0)
        parts = (
            turn(0, 2, psum_x, "xt_v", "xt_s"),
            turn(2, 3, psum_x, "xt_v", "xt_s"),
            turn(3, 4, psum_z, "z", "z"),
        )
        first, second, third = parts
        for part in parts:
            square_of(*part)
        deviation_of(*first)
        deviation_of(*second)
        at_least_zero(*first)
        root_of(*first)
        deviation_of(*third)
        at_least_zero(*second)
        root_of(*second)
        at_least_zero(*third)
        root_of(*third)
        for part in parts:
            mean_of(*part)
